import numpy as np
import ml_dtypes


def mxq(x, axis, fmt="e4m3"):
    dtype, down = {"e4m3": (ml_dtypes.float8_e4m3fn, 7), "e5m2": (ml_dtypes.float8_e5m2, 14)}[fmt]
    v = np.moveaxis(np.asarray(x, np.float32).astype(ml_dtypes.bfloat16).astype(np.float64), axis, -1)
    blocks = v.reshape(v.shape[:-1] + (-1, 32))
    amax = np.abs(blocks).max(-1, keepdims=True)
    byte = np.maximum(np.where(amax > 0, np.frexp(amax)[1] - 1 + 127, 0) - down, 1)
    scale = np.exp2(byte - 127.0)
    codes = (blocks / scale).astype(np.float32).astype(dtype).astype(np.float64)
    return np.moveaxis((codes * scale).reshape(v.shape), -1, axis)


WIDE = False


def mx_kscale(k):
    if not WIDE:
        return np.ones(k)
    levels = np.array([20, -20, 10, -10, 0])
    a = np.random.permutation(np.resize(levels, k // 512 * 4)).reshape(k // 512, 4)
    idx = np.arange(k)
    return np.exp2(a[idx // 512, idx % 128 // 32])


BF16 = ml_dtypes.bfloat16


def bf(x):
    return np.asarray(x, np.float32).astype(BF16)


def f64(x):
    return np.asarray(x).astype(np.float64)


B, T, N, C, WIN, F = 1, 4, 512, 512, 3, 3
NW = T - WIN + 1


def sigmoid(v):
    return 1.0 / (1.0 + np.exp(-v))


def setup_inputs():
    u = mx_kscale(C)
    agg = bf(np.random.standard_normal((B, NW, N, C)))
    W0 = bf(np.random.standard_normal((NW, F, C, 2 * C)) / np.sqrt(C))
    b = bf(np.random.standard_normal((NW, F, 2 * C)) * 0.3)
    g = bf(np.random.standard_normal((B, NW, N, C)) * np.exp2(np.random.randint(-12, 1, (B, NW, N, 1))) * 8.0 * u)
    pre = f64(agg)[:, :, None] @ f64(W0) + f64(b)[None, :, :, None, :]
    W = bf(f64(W0) / np.concatenate([u, u]))
    return {"agg": agg, "W": W, "b": b, "pre": np.asarray(pre, np.float32), "grad_out": g}


def reference(agg, W, b, pre, grad_out):
    p = f64(pre)
    lhs, rhs = p[..., :C], p[..., C:]
    sg = sigmoid(rhs)
    glu = lhs * sg
    top = glu.max(axis=2, keepdims=True)
    hit = np.where(glu == top, 1.0, 0.0)
    hit = hit / hit.sum(axis=2, keepdims=True)
    dg = f64(grad_out)[:, :, None] * hit
    dpre = np.concatenate([dg * sg, dg * lhs * sg * (1.0 - sg)], axis=-1)
    dflat = dpre.transpose(0, 1, 3, 2, 4).reshape(B, NW, N, F * 2 * C)
    wflat = f64(W).transpose(0, 2, 1, 3).reshape(NW, C, F * 2 * C)
    dq = mxq(dflat, 3, "e5m2")
    wq = mxq(wflat, 2, "e4m3")
    return dq @ wq.transpose(0, 2, 1)[None]

@@ -1,0 +1,169 @@
+from contextlib import ExitStack
+
+import concourse.mybir as mybir
+from concourse.masks import make_identity
+
+F32 = mybir.dt.float32
+BF16 = mybir.dt.bfloat16
+U32 = mybir.dt.uint32
+U8 = mybir.dt.uint8
+E4M3X4 = mybir.dt.float8_e4m3fn_x4
+E5M2X4 = mybir.dt.float8_e5m2_x4
+ALU = mybir.AluOpType
+ACT = mybir.ActivationFunctionType
+
+P = 128
+PACK = 4
+WINDOWS = 2
+BRANCHES = 3
+NODES = 512
+C = 512
+HALVES = 2
+PASSES = BRANCHES * HALVES
+NODE_TILES = NODES // P
+CH_TILES = C // P
+UNITS = WINDOWS * NODE_TILES
+AHEAD = 2
+
+FLOPS = 2 * WINDOWS * NODES * C * BRANCHES * 2 * C
+BYTES = WINDOWS * (BRANCHES * NODES * 2 * C * 4 + BRANCHES * C * 2 * C * 2 + NODES * C * 2 + NODES * C * 4)
+
+
+def tile_stsindividuallayer_pb_v_kernel(tc, agg, W, b, pre, grad_out, out):
+    nc = tc.nc
+    with ExitStack() as pools:
+        keep = pools.enter_context(tc.tile_pool(name="keep", bufs=1))
+        pre_in = pools.enter_context(tc.tile_pool(name="pre_in", bufs=AHEAD + 1))
+        w_in = pools.enter_context(tc.tile_pool(name="w_in", bufs=BRANCHES))
+        work = pools.enter_context(tc.tile_pool(name="work", bufs=2))
+        mx = pools.enter_context(tc.tile_pool(name="mx", bufs=3))
+        flipped = pools.enter_context(tc.psum_pool(name="flipped", bufs=4))
+        sums = pools.enter_context(tc.psum_pool(name="sums", bufs=2))
+        ident = keep.tile([P, P], BF16)
+        make_identity(nc, ident[:])
+        grad = keep.tile([P, UNITS, C], BF16)
+        w_codes = keep.tile([P, WINDOWS * PASSES, C], U32, align_bytes=64)
+        w_scales = keep.tile([P, WINDOWS * PASSES, C], U8, align_bytes=64)
+        pre_tiles = {}
+        w_tiles = {}
+
+        def load_pre(u):
+            w, rows = u // NODE_TILES, slice((u % NODE_TILES) * P, (u % NODE_TILES + 1) * P)
+            pre_t = pre_in.tile([P, BRANCHES, 2 * C], F32)
+            nc.sync.dma_start(out=pre_t[:], in_=pre[0, w, :, rows, :].rearrange("f p j -> p f j"))
+            pre_tiles[u] = pre_t
+
+        def load_w(w):
+            for f in range(BRANCHES):
+                w_raw = w_in.tile([P, CH_TILES, 2 * C], BF16)
+                nc.sync.dma_start(out=w_raw[:], in_=W[w, f].rearrange("(a p) j -> p a j", p=P))
+                w_tiles[(w, f)] = w_raw
+
+        def quantise_w(w):
+            for f in range(BRANCHES):
+                w_raw = w_tiles[(w, f)]
+                for h in range(HALVES):
+                    w_grouped = work.tile([P, C, PACK], BF16, align_bytes=64)
+                    for pair in range(CH_TILES // 2):
+                        w_flip = flipped.tile([P, 2, PACK, P], BF16, tag="flip")
+                        for a in range(2):
+                            for t in range(PACK):
+                                j0 = h * C + t * P
+                                nc.tensor.transpose(w_flip[:, a, t, :], w_raw[:, 2 * pair + a, j0 : j0 + P], ident[:])
+                        nc.scalar.copy(
+                            out=w_grouped[:, 2 * pair * P : (2 * pair + 2) * P, :].rearrange("p (a c) t -> p a c t", a=2),
+                            in_=w_flip[:].rearrange("p a t c -> p a c t"),
+                        )
+                    s = w * PASSES + f * HALVES + h
+                    nc.vector.quantize_mx(
+                        out=w_codes[:, s, :].bitcast(E4M3X4),
+                        scales=w_scales[:, s, :],
+                        in_=w_grouped[:].rearrange("p c t -> p (c t)"),
+                    )
+
+        def gate(u):
+            pre_t = pre_tiles[u]
+            lhs = pre_t[:, :, 0:C]
+            rhs = pre_t[:, :, C : 2 * C]
+            sg = work.tile([P, BRANCHES, C], F32)
+            nc.scalar.activation(out=sg[:], in_=rhs, func=ACT.Sigmoid)
+            glu = work.tile([P, BRANCHES, C], F32)
+            nc.vector.tensor_tensor(out=glu[:], in0=lhs, in1=sg[:], op=ALU.mult)
+            top = work.tile([P, C], F32)
+            nc.vector.tensor_tensor(out=top[:], in0=glu[:, 0, :], in1=glu[:, 1, :], op=ALU.max)
+            nc.vector.tensor_tensor(out=top[:], in0=top[:], in1=glu[:, 2, :], op=ALU.max)
+            won = work.tile([P, BRANCHES, C], BF16)
+            nc.vector.tensor_tensor(
+                out=won[:], in0=glu[:], in1=top[:].unsqueeze(1).to_broadcast([P, BRANCHES, C]), op=ALU.is_equal
+            )
+            count = work.tile([P, C], BF16)
+            nc.vector.tensor_tensor(out=count[:], in0=won[:, 0, :], in1=won[:, 1, :], op=ALU.add)
+            nc.vector.tensor_tensor(out=count[:], in0=count[:], in1=won[:, 2, :], op=ALU.add)
+            line = work.tile([P, C], BF16)
+            nc.vector.tensor_scalar(out=line[:], in0=count[:], scalar1=-0.5, scalar2=1.5, op0=ALU.mult, op1=ALU.add)
+            share = work.tile([P, C], F32)
+            nc.vector.scalar_tensor_tensor(
+                out=share[:], in0=line[:], scalar=1.0 / 3.0, in1=grad[:, u, :], op0=ALU.max, op1=ALU.mult
+            )
+            dg = work.tile([P, BRANCHES, C], F32)
+            nc.vector.tensor_tensor(
+                out=dg[:], in0=won[:], in1=share[:].unsqueeze(1).to_broadcast([P, BRANCHES, C]), op=ALU.mult
+            )
+            dpre = work.tile([P, BRANCHES, HALVES, C], BF16)
+            nc.vector.tensor_tensor(out=dpre[:, :, 0, :], in0=dg[:], in1=sg[:], op=ALU.mult)
+            minus = work.tile([P, BRANCHES, C], F32)
+            nc.vector.scalar_tensor_tensor(out=minus[:], in0=sg[:], scalar=1.0, in1=glu[:], op0=ALU.subtract, op1=ALU.mult)
+            nc.vector.scalar_tensor_tensor(
+                out=dpre[:, :, 1, :], in0=minus[:], scalar=-1.0, in1=dg[:], op0=ALU.mult, op1=ALU.mult
+            )
+            return dpre
+
+        def quantise_dpre(dpre):
+            d_codes = mx.tile([P, PASSES, P], U32, align_bytes=64)
+            d_scales = mx.tile([P, PASSES, P], U8, align_bytes=64)
+            for f in range(BRANCHES):
+                d_flip = flipped.tile([P, HALVES, PACK, P], BF16, tag="flip")
+                for h in range(HALVES):
+                    for t in range(PACK):
+                        nc.tensor.transpose(d_flip[:, h, t, :], dpre[:, f, h, t * P : (t + 1) * P], ident[:])
+                d_grouped = mx.tile([P, HALVES, P, PACK], BF16, align_bytes=64)
+                nc.scalar.copy(out=d_grouped[:], in_=d_flip[:].rearrange("p h t n -> p h n t"))
+                both = slice(f * HALVES, (f + 1) * HALVES)
+                nc.vector.quantize_mx(
+                    out=d_codes[:, both, :].rearrange("p h n -> p (h n)").bitcast(E5M2X4),
+                    scales=d_scales[:, both, :].rearrange("p h n -> p (h n)"),
+                    in_=d_grouped[:].rearrange("p h n t -> p (h n t)"),
+                )
+            return d_codes, d_scales
+
+        def multiply(u, d_codes, d_scales):
+            w, rows = u // NODE_TILES, slice((u % NODE_TILES) * P, (u % NODE_TILES + 1) * P)
+            acc = sums.tile([P, C], F32)
+            for s in range(PASSES):
+                nc.tensor.matmul_mx(
+                    out=acc[:],
+                    lhsT=d_codes[:, s, :].bitcast(E5M2X4),
+                    lhsT_scale=d_scales[:, s, :],
+                    rhs=w_codes[:, w * PASSES + s, :].bitcast(E4M3X4),
+                    rhs_scale=w_scales[:, w * PASSES + s, :],
+                    start=(s == 0),
+                    stop=(s == PASSES - 1),
+                )
+            result = mx.tile([P, C], F32)
+            nc.scalar.copy(out=result[:], in_=acc[:])
+            nc.scalar.dma_start(out=out[0, w, rows, :], in_=result[:])
+
+        load_pre(0)
+        nc.sync.dma_start(out=grad[:], in_=grad_out[0].rearrange("w (a p) c -> p (w a) c", p=P))
+        load_w(0)
+        load_pre(1)
+        for u in range(UNITS):
+            if u + AHEAD < UNITS:
+                load_pre(u + AHEAD)
+            dpre = gate(u)
+            if u < WINDOWS:
+                quantise_w(u)
+                if u + 1 < WINDOWS:
+                    load_w(u + 1)
+            d_codes, d_scales = quantise_dpre(dpre)
+            multiply(u, d_codes, d_scales)

@@ -50,7 +50,8 @@ def tile_stsindividuallayer_pb_v_kernel(tc, agg, W, b, pre, grad_out, out):
         def load_pre(u):
             w, rows = u // NODE_TILES, slice((u % NODE_TILES) * P, (u % NODE_TILES + 1) * P)
             pre_t = pre_in.tile([P, BRANCHES, 2 * C], F32)
-            nc.sync.dma_start(out=pre_t[:], in_=pre[0, w, :, rows, :].rearrange("f p j -> p f j"))
+            for f in range(BRANCHES):
+                nc.sync.dma_start(out=pre_t[:, f, :], in_=pre[0, w, f, rows, :])
             pre_tiles[u] = pre_t
 
         def load_w(w):
@@ -81,21 +82,21 @@ def tile_stsindividuallayer_pb_v_kernel(tc, agg, W, b, pre, grad_out, out):
                         in_=w_grouped[:].rearrange("p c t -> p (c t)"),
                     )
 
+        def over_branches(plane):
+            return plane[:].unsqueeze(1).to_broadcast([P, BRANCHES, C])
+
         def gate(u):
             pre_t = pre_tiles[u]
-            lhs = pre_t[:, :, 0:C]
-            rhs = pre_t[:, :, C : 2 * C]
             sg = work.tile([P, BRANCHES, C], F32)
-            nc.scalar.activation(out=sg[:], in_=rhs, func=ACT.Sigmoid)
             glu = work.tile([P, BRANCHES, C], F32)
-            nc.vector.tensor_tensor(out=glu[:], in0=lhs, in1=sg[:], op=ALU.mult)
+            for f in range(BRANCHES):
+                nc.scalar.activation(out=sg[:, f, :], in_=pre_t[:, f, C : 2 * C], func=ACT.Sigmoid)
+                nc.vector.tensor_tensor(out=glu[:, f, :], in0=pre_t[:, f, 0:C], in1=sg[:, f, :], op=ALU.mult)
             top = work.tile([P, C], F32)
             nc.vector.tensor_tensor(out=top[:], in0=glu[:, 0, :], in1=glu[:, 1, :], op=ALU.max)
             nc.vector.tensor_tensor(out=top[:], in0=top[:], in1=glu[:, 2, :], op=ALU.max)
             won = work.tile([P, BRANCHES, C], BF16)
-            nc.vector.tensor_tensor(
-                out=won[:], in0=glu[:], in1=top[:].unsqueeze(1).to_broadcast([P, BRANCHES, C]), op=ALU.is_equal
-            )
+            nc.vector.tensor_tensor(out=won[:], in0=glu[:], in1=over_branches(top), op=ALU.is_equal)
             count = work.tile([P, C], BF16)
             nc.vector.tensor_tensor(out=count[:], in0=won[:, 0, :], in1=won[:, 1, :], op=ALU.add)
             nc.vector.tensor_tensor(out=count[:], in0=count[:], in1=won[:, 2, :], op=ALU.add)
@@ -105,17 +106,22 @@ def tile_stsindividuallayer_pb_v_kernel(tc, agg, W, b, pre, grad_out, out):
             nc.vector.scalar_tensor_tensor(
                 out=share[:], in0=line[:], scalar=1.0 / 3.0, in1=grad[:, u, :], op0=ALU.max, op1=ALU.mult
             )
-            dg = work.tile([P, BRANCHES, C], F32)
-            nc.vector.tensor_tensor(
-                out=dg[:], in0=won[:], in1=share[:].unsqueeze(1).to_broadcast([P, BRANCHES, C]), op=ALU.mult
+            minus_share_top = work.tile([P, C], F32)
+            nc.vector.scalar_tensor_tensor(
+                out=minus_share_top[:], in0=share[:], scalar=-1.0, in1=top[:], op0=ALU.mult, op1=ALU.mult
             )
             dpre = work.tile([P, BRANCHES, HALVES, C], BF16)
-            nc.vector.tensor_tensor(out=dpre[:, :, 0, :], in0=dg[:], in1=sg[:], op=ALU.mult)
-            minus = work.tile([P, BRANCHES, C], F32)
-            nc.vector.scalar_tensor_tensor(out=minus[:], in0=sg[:], scalar=1.0, in1=glu[:], op0=ALU.subtract, op1=ALU.mult)
+            nc.vector.tensor_tensor(out=dpre[:, :, 0, :], in0=sg[:], in1=over_branches(share), op=ALU.mult)
             nc.vector.scalar_tensor_tensor(
-                out=dpre[:, :, 1, :], in0=minus[:], scalar=-1.0, in1=dg[:], op0=ALU.mult, op1=ALU.mult
+                out=dpre[:, :, 1, :], in0=sg[:], scalar=1.0, in1=over_branches(minus_share_top), op0=ALU.subtract, op1=ALU.mult
             )
+            for f in range(BRANCHES):
+                nc.vector.tensor_tensor(
+                    out=dpre[:, f, :, :],
+                    in0=dpre[:, f, :, :],
+                    in1=won[:, f, :].unsqueeze(1).to_broadcast([P, HALVES, C]),
+                    op=ALU.mult,
+                )
             return dpre
 
         def quantise_dpre(dpre):

@@ -23,153 +23,257 @@ PASSES = BRANCHES * HALVES
 NODE_TILES = NODES // P
 CH_TILES = C // P
 UNITS = WINDOWS * NODE_TILES
-AHEAD = 2
+ROUNDS = UNITS + 2
+PRE_AHEAD = 3
+W_PASSES_A_ROUND = 3
 
 FLOPS = 2 * WINDOWS * NODES * C * BRANCHES * 2 * C
 BYTES = WINDOWS * (BRANCHES * NODES * 2 * C * 4 + BRANCHES * C * 2 * C * 2 + NODES * C * 2 + NODES * C * 4)
 
 
+def is_unit(u):
+    return 0 <= u < UNITS
+
+
+def window_and_rows(u):
+    return u // NODE_TILES, slice((u % NODE_TILES) * P, (u % NODE_TILES + 1) * P)
+
+
 def tile_stsindividuallayer_pb_v_kernel(tc, agg, W, b, pre, grad_out, out):
     nc = tc.nc
-    with ExitStack() as pools:
-        keep = pools.enter_context(tc.tile_pool(name="keep", bufs=1))
-        pre_in = pools.enter_context(tc.tile_pool(name="pre_in", bufs=AHEAD + 1))
-        w_in = pools.enter_context(tc.tile_pool(name="w_in", bufs=BRANCHES))
-        work = pools.enter_context(tc.tile_pool(name="work", bufs=2))
-        mx = pools.enter_context(tc.tile_pool(name="mx", bufs=3))
-        flipped = pools.enter_context(tc.psum_pool(name="flipped", bufs=4))
-        sums = pools.enter_context(tc.psum_pool(name="sums", bufs=2))
+    with ExitStack() as stack:
+        keep = stack.enter_context(tc.tile_pool(name="keep", bufs=1))
+        pre_in = stack.enter_context(tc.tile_pool(name="pre_in", bufs=PRE_AHEAD))
+        w_in = stack.enter_context(tc.tile_pool(name="w_in", bufs=WINDOWS * BRANCHES))
+        sig = stack.enter_context(tc.tile_pool(name="sig", bufs=3))
+        first = stack.enter_context(tc.tile_pool(name="first", bufs=2))
+        short = stack.enter_context(tc.tile_pool(name="short", bufs=1))
+        masked = stack.enter_context(tc.tile_pool(name="masked", bufs=2))
+        w_mid = stack.enter_context(tc.tile_pool(name="w_mid", bufs=2 * W_PASSES_A_ROUND))
+        d_mid = stack.enter_context(tc.tile_pool(name="d_mid", bufs=BRANCHES))
+        mx = stack.enter_context(tc.tile_pool(name="mx", bufs=2))
+        flipped = stack.enter_context(tc.psum_pool(name="flipped", bufs=6))
+        sums = stack.enter_context(tc.psum_pool(name="sums", bufs=2))
+
         ident = keep.tile([P, P], BF16)
         make_identity(nc, ident[:])
+        stack.enter_context(tc.manual_schedule())
         grad = keep.tile([P, UNITS, C], BF16)
         w_codes = keep.tile([P, WINDOWS * PASSES, C], U32, align_bytes=64)
         w_scales = keep.tile([P, WINDOWS * PASSES, C], U8, align_bytes=64)
-        pre_tiles = {}
-        w_tiles = {}
+        pre_of, w_of, w_grouped_of = {}, {}, {}
+        sg_of, glu_of, top_of, won_of = {}, {}, {}, {}
+        count_of, line_of, share_of, minus_share_top_of, dpre_of = {}, {}, {}, {}, {}
+        d_grouped_of, d_codes_of, d_scales_of = {}, {}, {}
 
         def load_pre(u):
-            w, rows = u // NODE_TILES, slice((u % NODE_TILES) * P, (u % NODE_TILES + 1) * P)
-            pre_t = pre_in.tile([P, BRANCHES, 2 * C], F32)
-            for f in range(BRANCHES):
-                nc.sync.dma_start(out=pre_t[:, f, :], in_=pre[0, w, f, rows, :])
-            pre_tiles[u] = pre_t
+            if is_unit(u):
+                w, rows = window_and_rows(u)
+                pre_t = pre_in.tile([P, BRANCHES, 2 * C], F32)
+                for f in range(BRANCHES):
+                    nc.sync.dma_start(out=pre_t[:, f, :], in_=pre[0, w, f, rows, :])
+                pre_of[u] = pre_t
 
-        def load_w(w):
-            for f in range(BRANCHES):
-                w_raw = w_in.tile([P, CH_TILES, 2 * C], BF16)
-                nc.sync.dma_start(out=w_raw[:], in_=W[w, f].rearrange("(a p) j -> p a j", p=P))
-                w_tiles[(w, f)] = w_raw
+        def load_w(w, f):
+            w_raw = w_in.tile([P, CH_TILES, 2 * C], BF16)
+            nc.sync.dma_start(out=w_raw[:], in_=W[w, f].rearrange("(a p) j -> p a j", p=P))
+            w_of[(w, f)] = w_raw
 
-        def quantise_w(w):
-            for f in range(BRANCHES):
-                w_raw = w_tiles[(w, f)]
-                for h in range(HALVES):
-                    w_grouped = work.tile([P, C, PACK], BF16, align_bytes=64)
-                    for pair in range(CH_TILES // 2):
-                        w_flip = flipped.tile([P, 2, PACK, P], BF16, tag="flip")
-                        for a in range(2):
-                            for t in range(PACK):
-                                j0 = h * C + t * P
-                                nc.tensor.transpose(w_flip[:, a, t, :], w_raw[:, 2 * pair + a, j0 : j0 + P], ident[:])
-                        nc.scalar.copy(
-                            out=w_grouped[:, 2 * pair * P : (2 * pair + 2) * P, :].rearrange("p (a c) t -> p a c t", a=2),
-                            in_=w_flip[:].rearrange("p a t c -> p a c t"),
-                        )
-                    s = w * PASSES + f * HALVES + h
-                    nc.vector.quantize_mx(
-                        out=w_codes[:, s, :].bitcast(E4M3X4),
-                        scales=w_scales[:, s, :],
-                        in_=w_grouped[:].rearrange("p c t -> p (c t)"),
-                    )
+        def w_passes_of_round(r):
+            return [s for s in range(r * W_PASSES_A_ROUND, (r + 1) * W_PASSES_A_ROUND) if 0 <= s < WINDOWS * PASSES]
+
+        def flip_w(s):
+            w_raw = w_of[(s // PASSES, (s % PASSES) // HALVES)]
+            h = s % HALVES
+            w_grouped = w_mid.tile([P, C, PACK], BF16, align_bytes=64)
+            for pair in range(CH_TILES // 2):
+                w_flip = flipped.tile([P, 2, PACK, P], BF16, tag="flip")
+                for a in range(2):
+                    for t in range(PACK):
+                        j0 = h * C + t * P
+                        nc.tensor.transpose(w_flip[:, a, t, :], w_raw[:, 2 * pair + a, j0 : j0 + P], ident[:])
+                nc.scalar.copy(
+                    out=w_grouped[:, 2 * pair * P : (2 * pair + 2) * P, :].rearrange("p (a c) t -> p a c t", a=2),
+                    in_=w_flip[:].rearrange("p a t c -> p a c t"),
+                )
+            w_grouped_of[s] = w_grouped
+
+        def quantise_w(s):
+            nc.vector.quantize_mx(
+                out=w_codes[:, s, :].bitcast(E4M3X4),
+                scales=w_scales[:, s, :],
+                in_=w_grouped_of[s][:].rearrange("p c t -> p (c t)"),
+            )
 
         def over_branches(plane):
             return plane[:].unsqueeze(1).to_broadcast([P, BRANCHES, C])
 
-        def gate(u):
-            pre_t = pre_tiles[u]
-            sg = work.tile([P, BRANCHES, C], F32)
-            glu = work.tile([P, BRANCHES, C], F32)
-            for f in range(BRANCHES):
-                nc.scalar.activation(out=sg[:, f, :], in_=pre_t[:, f, C : 2 * C], func=ACT.Sigmoid)
-                nc.vector.tensor_tensor(out=glu[:, f, :], in0=pre_t[:, f, 0:C], in1=sg[:, f, :], op=ALU.mult)
-            top = work.tile([P, C], F32)
-            nc.vector.tensor_tensor(out=top[:], in0=glu[:, 0, :], in1=glu[:, 1, :], op=ALU.max)
-            nc.vector.tensor_tensor(out=top[:], in0=top[:], in1=glu[:, 2, :], op=ALU.max)
-            won = work.tile([P, BRANCHES, C], BF16)
-            nc.vector.tensor_tensor(out=won[:], in0=glu[:], in1=over_branches(top), op=ALU.is_equal)
-            count = work.tile([P, C], BF16)
-            nc.vector.tensor_tensor(out=count[:], in0=won[:, 0, :], in1=won[:, 1, :], op=ALU.add)
-            nc.vector.tensor_tensor(out=count[:], in0=count[:], in1=won[:, 2, :], op=ALU.add)
-            line = work.tile([P, C], BF16)
-            nc.vector.tensor_scalar(out=line[:], in0=count[:], scalar1=-0.5, scalar2=1.5, op0=ALU.mult, op1=ALU.add)
-            share = work.tile([P, C], F32)
-            nc.vector.scalar_tensor_tensor(
-                out=share[:], in0=line[:], scalar=1.0 / 3.0, in1=grad[:, u, :], op0=ALU.max, op1=ALU.mult
-            )
-            minus_share_top = work.tile([P, C], F32)
-            nc.vector.scalar_tensor_tensor(
-                out=minus_share_top[:], in0=share[:], scalar=-1.0, in1=top[:], op0=ALU.mult, op1=ALU.mult
-            )
-            dpre = work.tile([P, BRANCHES, HALVES, C], BF16)
-            nc.vector.tensor_tensor(out=dpre[:, :, 0, :], in0=sg[:], in1=over_branches(share), op=ALU.mult)
-            nc.vector.scalar_tensor_tensor(
-                out=dpre[:, :, 1, :], in0=sg[:], scalar=1.0, in1=over_branches(minus_share_top), op0=ALU.subtract, op1=ALU.mult
-            )
-            for f in range(BRANCHES):
+        def sigmoid(u):
+            if is_unit(u):
+                sg = sig.tile([P, BRANCHES, C], F32)
+                for f in range(BRANCHES):
+                    nc.scalar.activation(out=sg[:, f, :], in_=pre_of[u][:, f, C : 2 * C], func=ACT.Sigmoid)
+                sg_of[u] = sg
+
+        def glu_of_branch(u, f):
+            if is_unit(u):
+                if f == 0:
+                    glu = first.tile([P, BRANCHES, C], F32)
+                    glu_of[u] = glu
+                nc.vector.tensor_tensor(
+                    out=glu_of[u][:, f, :], in0=pre_of[u][:, f, 0:C], in1=sg_of[u][:, f, :], op=ALU.mult
+                )
+
+        def top_of_two(u):
+            if is_unit(u):
+                top = first.tile([P, C], F32)
+                nc.vector.tensor_tensor(out=top[:], in0=glu_of[u][:, 0, :], in1=glu_of[u][:, 1, :], op=ALU.max)
+                top_of[u] = top
+
+        def top_of_three(u):
+            if is_unit(u):
+                nc.vector.tensor_tensor(out=top_of[u][:], in0=top_of[u][:], in1=glu_of[u][:, 2, :], op=ALU.max)
+
+        def winners(u):
+            if is_unit(u):
+                won = first.tile([P, BRANCHES, C], BF16)
+                nc.vector.tensor_tensor(out=won[:], in0=glu_of[u][:], in1=over_branches(top_of[u]), op=ALU.is_equal)
+                won_of[u] = won
+
+        def count_two(u):
+            if is_unit(u):
+                count = short.tile([P, C], BF16)
+                nc.vector.tensor_tensor(out=count[:], in0=won_of[u][:, 0, :], in1=won_of[u][:, 1, :], op=ALU.add)
+                count_of[u] = count
+
+        def count_three(u):
+            if is_unit(u):
+                nc.vector.tensor_tensor(out=count_of[u][:], in0=count_of[u][:], in1=won_of[u][:, 2, :], op=ALU.add)
+
+        def line_of_count(u):
+            if is_unit(u):
+                line = short.tile([P, C], BF16)
+                nc.vector.tensor_scalar(
+                    out=line[:], in0=count_of[u][:], scalar1=-0.5, scalar2=1.5, op0=ALU.mult, op1=ALU.add
+                )
+                line_of[u] = line
+
+        def share_of_grad(u):
+            if is_unit(u):
+                share = short.tile([P, C], F32)
+                nc.vector.scalar_tensor_tensor(
+                    out=share[:], in0=line_of[u][:], scalar=1.0 / 3.0, in1=grad[:, u, :], op0=ALU.max, op1=ALU.mult
+                )
+                share_of[u] = share
+
+        def share_times_top(u):
+            if is_unit(u):
+                minus_share_top = short.tile([P, C], F32)
+                nc.vector.scalar_tensor_tensor(
+                    out=minus_share_top[:], in0=share_of[u][:], scalar=-1.0, in1=top_of[u][:], op0=ALU.mult, op1=ALU.mult
+                )
+                minus_share_top_of[u] = minus_share_top
+
+        def lhs_half(u):
+            if is_unit(u):
+                dpre = masked.tile([P, BRANCHES, HALVES, C], BF16)
+                nc.vector.tensor_tensor(out=dpre[:, :, 0, :], in0=sg_of[u][:], in1=over_branches(share_of[u]), op=ALU.mult)
+                dpre_of[u] = dpre
+
+        def rhs_half(u):
+            if is_unit(u):
+                nc.vector.scalar_tensor_tensor(
+                    out=dpre_of[u][:, :, 1, :],
+                    in0=sg_of[u][:],
+                    scalar=1.0,
+                    in1=over_branches(minus_share_top_of[u]),
+                    op0=ALU.subtract,
+                    op1=ALU.mult,
+                )
+
+        def mask_and_flip(u, f):
+            if is_unit(u):
+                dpre = dpre_of[u]
                 nc.vector.tensor_tensor(
                     out=dpre[:, f, :, :],
                     in0=dpre[:, f, :, :],
-                    in1=won[:, f, :].unsqueeze(1).to_broadcast([P, HALVES, C]),
+                    in1=won_of[u][:, f, :].unsqueeze(1).to_broadcast([P, HALVES, C]),
                     op=ALU.mult,
                 )
-            return dpre
-
-        def quantise_dpre(dpre):
-            d_codes = mx.tile([P, PASSES, P], U32, align_bytes=64)
-            d_scales = mx.tile([P, PASSES, P], U8, align_bytes=64)
-            for f in range(BRANCHES):
                 d_flip = flipped.tile([P, HALVES, PACK, P], BF16, tag="flip")
                 for h in range(HALVES):
                     for t in range(PACK):
                         nc.tensor.transpose(d_flip[:, h, t, :], dpre[:, f, h, t * P : (t + 1) * P], ident[:])
-                d_grouped = mx.tile([P, HALVES, P, PACK], BF16, align_bytes=64)
+                d_grouped = d_mid.tile([P, HALVES, P, PACK], BF16, align_bytes=64)
                 nc.scalar.copy(out=d_grouped[:], in_=d_flip[:].rearrange("p h t n -> p h n t"))
+                d_grouped_of[(u, f)] = d_grouped
+
+        def quantise_branch(u, f):
+            if is_unit(u):
+                if f == 0:
+                    d_codes = mx.tile([P, PASSES, P], U32, align_bytes=64)
+                    d_scales = mx.tile([P, PASSES, P], U8, align_bytes=64)
+                    d_codes_of[u], d_scales_of[u] = d_codes, d_scales
                 both = slice(f * HALVES, (f + 1) * HALVES)
                 nc.vector.quantize_mx(
-                    out=d_codes[:, both, :].rearrange("p h n -> p (h n)").bitcast(E5M2X4),
-                    scales=d_scales[:, both, :].rearrange("p h n -> p (h n)"),
-                    in_=d_grouped[:].rearrange("p h n t -> p (h n t)"),
+                    out=d_codes_of[u][:, both, :].rearrange("p h n -> p (h n)").bitcast(E5M2X4),
+                    scales=d_scales_of[u][:, both, :].rearrange("p h n -> p (h n)"),
+                    in_=d_grouped_of[(u, f)][:].rearrange("p h n t -> p (h n t)"),
                 )
-            return d_codes, d_scales
 
-        def multiply(u, d_codes, d_scales):
-            w, rows = u // NODE_TILES, slice((u % NODE_TILES) * P, (u % NODE_TILES + 1) * P)
-            acc = sums.tile([P, C], F32)
-            for s in range(PASSES):
-                nc.tensor.matmul_mx(
-                    out=acc[:],
-                    lhsT=d_codes[:, s, :].bitcast(E5M2X4),
-                    lhsT_scale=d_scales[:, s, :],
-                    rhs=w_codes[:, w * PASSES + s, :].bitcast(E4M3X4),
-                    rhs_scale=w_scales[:, w * PASSES + s, :],
-                    start=(s == 0),
-                    stop=(s == PASSES - 1),
-                )
-            result = mx.tile([P, C], F32)
-            nc.scalar.copy(out=result[:], in_=acc[:])
-            nc.scalar.dma_start(out=out[0, w, rows, :], in_=result[:])
+        def multiply(u):
+            if is_unit(u):
+                w, rows = window_and_rows(u)
+                acc = sums.tile([P, C], F32)
+                for s in range(PASSES):
+                    nc.tensor.matmul_mx(
+                        out=acc[:],
+                        lhsT=d_codes_of[u][:, s, :].bitcast(E5M2X4),
+                        lhsT_scale=d_scales_of[u][:, s, :],
+                        rhs=w_codes[:, w * PASSES + s, :].bitcast(E4M3X4),
+                        rhs_scale=w_scales[:, w * PASSES + s, :],
+                        start=(s == 0),
+                        stop=(s == PASSES - 1),
+                    )
+                result = mx.tile([P, C], F32)
+                nc.scalar.copy(out=result[:], in_=acc[:])
+                nc.scalar.dma_start(out=out[0, w, rows, :], in_=result[:])
 
         load_pre(0)
-        nc.sync.dma_start(out=grad[:], in_=grad_out[0].rearrange("w (a p) c -> p (w a) c", p=P))
-        load_w(0)
         load_pre(1)
-        for u in range(UNITS):
-            if u + AHEAD < UNITS:
-                load_pre(u + AHEAD)
-            dpre = gate(u)
-            if u < WINDOWS:
-                quantise_w(u)
-                if u + 1 < WINDOWS:
-                    load_w(u + 1)
-            d_codes, d_scales = quantise_dpre(dpre)
-            multiply(u, d_codes, d_scales)
+        nc.sync.dma_start(out=grad[:], in_=grad_out[0].rearrange("w (a p) c -> p (w a) c", p=P))
+        load_w(0, 0)
+        load_w(0, 1)
+        load_pre(2)
+        load_w(0, 2)
+        sigmoid(0)
+        for r in range(ROUNDS):
+            begun, shared, done = r, r - 1, r - 2
+            sigmoid(begun + 1)
+            for s in w_passes_of_round(r):
+                flip_w(s)
+            glu_of_branch(begun, 0)
+            count_two(shared)
+            glu_of_branch(begun, 1)
+            count_three(shared)
+            glu_of_branch(begun, 2)
+            line_of_count(shared)
+            top_of_two(begun)
+            share_of_grad(shared)
+            top_of_three(begun)
+            share_times_top(shared)
+            winners(begun)
+            load_pre(begun + PRE_AHEAD)
+            if r == 0:
+                for f in range(BRANCHES):
+                    load_w(1, f)
+            lhs_half(shared)
+            quantise_branch(done, 0)
+            rhs_half(shared)
+            quantise_branch(done, 1)
+            quantise_branch(done, 2)
+            for f in range(BRANCHES):
+                mask_and_flip(shared, f)
+            for s in w_passes_of_round(r - 1):
+                quantise_w(s)
+            multiply(done)

@@ -23,9 +23,12 @@ PASSES = BRANCHES * HALVES
 NODE_TILES = NODES // P
 CH_TILES = C // P
 UNITS = WINDOWS * NODE_TILES
-ROUNDS = UNITS + 2
-PRE_AHEAD = 3
-W_PASSES_A_ROUND = 3
+PRE_TILES = 3
+W_BANKS = WINDOWS * PASSES * 2
+W_BANKS_A_ROUND = 6
+FIRST_W_ROUND = 2
+MULTIPLY_AFTER = 4
+ROUNDS = UNITS + MULTIPLY_AFTER
 
 FLOPS = 2 * WINDOWS * NODES * C * BRANCHES * 2 * C
 BYTES = WINDOWS * (BRANCHES * NODES * 2 * C * 4 + BRANCHES * C * 2 * C * 2 + NODES * C * 2 + NODES * C * 4)
@@ -43,28 +46,31 @@ def tile_stsindividuallayer_pb_v_kernel(tc, agg, W, b, pre, grad_out, out):
     nc = tc.nc
     with ExitStack() as stack:
         keep = stack.enter_context(tc.tile_pool(name="keep", bufs=1))
-        pre_in = stack.enter_context(tc.tile_pool(name="pre_in", bufs=PRE_AHEAD))
+        pre_in = stack.enter_context(tc.tile_pool(name="pre_in", bufs=PRE_TILES))
         w_in = stack.enter_context(tc.tile_pool(name="w_in", bufs=WINDOWS * BRANCHES))
         sig = stack.enter_context(tc.tile_pool(name="sig", bufs=3))
-        first = stack.enter_context(tc.tile_pool(name="first", bufs=2))
-        short = stack.enter_context(tc.tile_pool(name="short", bufs=1))
-        masked = stack.enter_context(tc.tile_pool(name="masked", bufs=2))
-        w_mid = stack.enter_context(tc.tile_pool(name="w_mid", bufs=2 * W_PASSES_A_ROUND))
-        d_mid = stack.enter_context(tc.tile_pool(name="d_mid", bufs=BRANCHES))
-        mx = stack.enter_context(tc.tile_pool(name="mx", bufs=2))
-        flipped = stack.enter_context(tc.psum_pool(name="flipped", bufs=6))
-        sums = stack.enter_context(tc.psum_pool(name="sums", bufs=2))
+        single = stack.enter_context(tc.tile_pool(name="single", bufs=1))
+        double = stack.enter_context(tc.tile_pool(name="double", bufs=2))
+        w_mid = stack.enter_context(tc.tile_pool(name="w_mid", bufs=W_BANKS_A_ROUND))
+        mx = stack.enter_context(tc.tile_pool(name="mx", bufs=MULTIPLY_AFTER - 1))
+        sg_banks = stack.enter_context(tc.psum_pool(name="sg_banks", bufs=BRANCHES))
+        flipped = stack.enter_context(tc.psum_pool(name="flipped", bufs=4))
+        sums = stack.enter_context(tc.psum_pool(name="sums", bufs=1))
 
         ident = keep.tile([P, P], BF16)
         make_identity(nc, ident[:])
+        ident_f32 = keep.tile([P, P], F32)
+        make_identity(nc, ident_f32[:])
         stack.enter_context(tc.manual_schedule())
+
         grad = keep.tile([P, UNITS, C], BF16)
         w_codes = keep.tile([P, WINDOWS * PASSES, C], U32, align_bytes=64)
         w_scales = keep.tile([P, WINDOWS * PASSES, C], U8, align_bytes=64)
         pre_of, w_of, w_grouped_of = {}, {}, {}
         sg_of, glu_of, top_of, won_of = {}, {}, {}, {}
-        count_of, line_of, share_of, minus_share_top_of, dpre_of = {}, {}, {}, {}, {}
-        d_grouped_of, d_codes_of, d_scales_of = {}, {}, {}
+        count_of, line_of, share_of, minus_share_top_of = {}, {}, {}, {}
+        sg_flipped_of, share_flipped_of, minus_share_top_flipped_of, won_flipped_of = {}, {}, {}, {}
+        dpre_of, d_codes_of, d_scales_of = {}, {}, {}
 
         def load_pre(u):
             if is_unit(u):
@@ -74,39 +80,37 @@ def tile_stsindividuallayer_pb_v_kernel(tc, agg, W, b, pre, grad_out, out):
                     nc.sync.dma_start(out=pre_t[:, f, :], in_=pre[0, w, f, rows, :])
                 pre_of[u] = pre_t
 
-        def load_w(w, f):
-            w_raw = w_in.tile([P, CH_TILES, 2 * C], BF16)
-            nc.sync.dma_start(out=w_raw[:], in_=W[w, f].rearrange("(a p) j -> p a j", p=P))
-            w_of[(w, f)] = w_raw
+        def load_w(w):
+            if w < WINDOWS:
+                for f in range(BRANCHES):
+                    w_raw = w_in.tile([P, CH_TILES, 2 * C], BF16)
+                    nc.sync.dma_start(out=w_raw[:], in_=W[w, f].rearrange("(a p) j -> p a j", p=P))
+                    w_of[(w, f)] = w_raw
 
-        def w_passes_of_round(r):
-            return [s for s in range(r * W_PASSES_A_ROUND, (r + 1) * W_PASSES_A_ROUND) if 0 <= s < WINDOWS * PASSES]
-
-        def flip_w(s):
-            w_raw = w_of[(s // PASSES, (s % PASSES) // HALVES)]
-            h = s % HALVES
-            w_grouped = w_mid.tile([P, C, PACK], BF16, align_bytes=64)
-            for pair in range(CH_TILES // 2):
+        def flip_w_bank(k):
+            if 0 <= k < W_BANKS:
+                s, pair = k // 2, k % 2
+                w_raw = w_of[(s // PASSES, (s % PASSES) // HALVES)]
+                if pair == 0:
+                    w_grouped = w_mid.tile([P, C, PACK], BF16, align_bytes=64)
+                    w_grouped_of[s] = w_grouped
                 w_flip = flipped.tile([P, 2, PACK, P], BF16, tag="flip")
                 for a in range(2):
                     for t in range(PACK):
-                        j0 = h * C + t * P
+                        j0 = (s % HALVES) * C + t * P
                         nc.tensor.transpose(w_flip[:, a, t, :], w_raw[:, 2 * pair + a, j0 : j0 + P], ident[:])
                 nc.scalar.copy(
-                    out=w_grouped[:, 2 * pair * P : (2 * pair + 2) * P, :].rearrange("p (a c) t -> p a c t", a=2),
+                    out=w_grouped_of[s][:, 2 * pair * P : (2 * pair + 2) * P, :].rearrange("p (a c) t -> p a c t", a=2),
                     in_=w_flip[:].rearrange("p a t c -> p a c t"),
                 )
-            w_grouped_of[s] = w_grouped
 
         def quantise_w(s):
-            nc.vector.quantize_mx(
-                out=w_codes[:, s, :].bitcast(E4M3X4),
-                scales=w_scales[:, s, :],
-                in_=w_grouped_of[s][:].rearrange("p c t -> p (c t)"),
-            )
-
-        def over_branches(plane):
-            return plane[:].unsqueeze(1).to_broadcast([P, BRANCHES, C])
+            if 0 <= s < WINDOWS * PASSES:
+                nc.vector.quantize_mx(
+                    out=w_codes[:, s, :].bitcast(E4M3X4),
+                    scales=w_scales[:, s, :],
+                    in_=w_grouped_of[s][:].rearrange("p c t -> p (c t)"),
+                )
 
         def sigmoid(u):
             if is_unit(u):
@@ -115,18 +119,16 @@ def tile_stsindividuallayer_pb_v_kernel(tc, agg, W, b, pre, grad_out, out):
                     nc.scalar.activation(out=sg[:, f, :], in_=pre_of[u][:, f, C : 2 * C], func=ACT.Sigmoid)
                 sg_of[u] = sg
 
-        def glu_of_branch(u, f):
+        def glu_of_branch(engine, u, f):
             if is_unit(u):
                 if f == 0:
-                    glu = first.tile([P, BRANCHES, C], F32)
+                    glu = single.tile([P, BRANCHES, C], F32)
                     glu_of[u] = glu
-                nc.vector.tensor_tensor(
-                    out=glu_of[u][:, f, :], in0=pre_of[u][:, f, 0:C], in1=sg_of[u][:, f, :], op=ALU.mult
-                )
+                engine.tensor_tensor(out=glu_of[u][:, f, :], in0=pre_of[u][:, f, 0:C], in1=sg_of[u][:, f, :], op=ALU.mult)
 
         def top_of_two(u):
             if is_unit(u):
-                top = first.tile([P, C], F32)
+                top = double.tile([P, C], F32)
                 nc.vector.tensor_tensor(out=top[:], in0=glu_of[u][:, 0, :], in1=glu_of[u][:, 1, :], op=ALU.max)
                 top_of[u] = top
 
@@ -136,13 +138,15 @@ def tile_stsindividuallayer_pb_v_kernel(tc, agg, W, b, pre, grad_out, out):
 
         def winners(u):
             if is_unit(u):
-                won = first.tile([P, BRANCHES, C], BF16)
-                nc.vector.tensor_tensor(out=won[:], in0=glu_of[u][:], in1=over_branches(top_of[u]), op=ALU.is_equal)
+                won = double.tile([P, BRANCHES, C], BF16)
+                nc.vector.tensor_tensor(
+                    out=won[:], in0=glu_of[u][:], in1=top_of[u][:].unsqueeze(1).to_broadcast([P, BRANCHES, C]), op=ALU.is_equal
+                )
                 won_of[u] = won
 
         def count_two(u):
             if is_unit(u):
-                count = short.tile([P, C], BF16)
+                count = single.tile([P, C], BF16)
                 nc.vector.tensor_tensor(out=count[:], in0=won_of[u][:, 0, :], in1=won_of[u][:, 1, :], op=ALU.add)
                 count_of[u] = count
 
@@ -152,7 +156,7 @@ def tile_stsindividuallayer_pb_v_kernel(tc, agg, W, b, pre, grad_out, out):
 
         def line_of_count(u):
             if is_unit(u):
-                line = short.tile([P, C], BF16)
+                line = single.tile([P, C], BF16)
                 nc.vector.tensor_scalar(
                     out=line[:], in0=count_of[u][:], scalar1=-0.5, scalar2=1.5, op0=ALU.mult, op1=ALU.add
                 )
@@ -160,7 +164,7 @@ def tile_stsindividuallayer_pb_v_kernel(tc, agg, W, b, pre, grad_out, out):
 
         def share_of_grad(u):
             if is_unit(u):
-                share = short.tile([P, C], F32)
+                share = single.tile([P, C], F32)
                 nc.vector.scalar_tensor_tensor(
                     out=share[:], in0=line_of[u][:], scalar=1.0 / 3.0, in1=grad[:, u, :], op0=ALU.max, op1=ALU.mult
                 )
@@ -168,45 +172,73 @@ def tile_stsindividuallayer_pb_v_kernel(tc, agg, W, b, pre, grad_out, out):
 
         def share_times_top(u):
             if is_unit(u):
-                minus_share_top = short.tile([P, C], F32)
+                minus_share_top = single.tile([P, C], F32)
                 nc.vector.scalar_tensor_tensor(
                     out=minus_share_top[:], in0=share_of[u][:], scalar=-1.0, in1=top_of[u][:], op0=ALU.mult, op1=ALU.mult
                 )
                 minus_share_top_of[u] = minus_share_top
 
-        def lhs_half(u):
+        def flip_sg(u):
             if is_unit(u):
-                dpre = masked.tile([P, BRANCHES, HALVES, C], BF16)
-                nc.vector.tensor_tensor(out=dpre[:, :, 0, :], in0=sg_of[u][:], in1=over_branches(share_of[u]), op=ALU.mult)
-                dpre_of[u] = dpre
+                for f in range(BRANCHES):
+                    sg_flipped = sg_banks.tile([P, PACK, P], F32)
+                    for t in range(PACK):
+                        nc.tensor.transpose(sg_flipped[:, t, :], sg_of[u][:, f, t * P : (t + 1) * P], ident_f32[:])
+                    sg_flipped_of[(u, f)] = sg_flipped
 
-        def rhs_half(u):
+        def flip_plane(plane, regrouped):
+            bank = flipped.tile([P, PACK, P], F32, tag="flip")
+            for t in range(PACK):
+                nc.tensor.transpose(bank[:, t, :], plane[:, t * P : (t + 1) * P], ident_f32[:])
+            nc.scalar.copy(out=regrouped[:], in_=bank[:].rearrange("p t n -> p n t"))
+
+        def flip_share(u):
             if is_unit(u):
+                share_flipped = single.tile([P, P, PACK], F32)
+                flip_plane(share_of[u], share_flipped)
+                share_flipped_of[u] = share_flipped
+
+        def flip_share_times_top(u):
+            if is_unit(u):
+                minus_share_top_flipped = single.tile([P, P, PACK], F32)
+                flip_plane(minus_share_top_of[u], minus_share_top_flipped)
+                minus_share_top_flipped_of[u] = minus_share_top_flipped
+
+        def flip_won(u):
+            if is_unit(u):
+                won_flipped = double.tile([P, BRANCHES, P, PACK], BF16)
+                for f in range(BRANCHES):
+                    bank = flipped.tile([P, PACK, P], BF16, tag="flip")
+                    for t in range(PACK):
+                        nc.tensor.transpose(bank[:, t, :], won_of[u][:, f, t * P : (t + 1) * P], ident[:])
+                    nc.scalar.copy(out=won_flipped[:, f, :, :], in_=bank[:].rearrange("p t n -> p n t"))
+                won_flipped_of[u] = won_flipped
+
+        def products(u, f):
+            if is_unit(u):
+                if f == 0:
+                    dpre = single.tile([P, BRANCHES, HALVES, P, PACK], BF16, align_bytes=64)
+                    dpre_of[u] = dpre
+                sg_by_node = sg_flipped_of[(u, f)][:].rearrange("p t n -> p n t")
+                nc.vector.tensor_tensor(out=dpre_of[u][:, f, 0, :, :], in0=sg_by_node, in1=share_flipped_of[u][:], op=ALU.mult)
                 nc.vector.scalar_tensor_tensor(
-                    out=dpre_of[u][:, :, 1, :],
-                    in0=sg_of[u][:],
+                    out=dpre_of[u][:, f, 1, :, :],
+                    in0=sg_by_node,
                     scalar=1.0,
-                    in1=over_branches(minus_share_top_of[u]),
+                    in1=minus_share_top_flipped_of[u][:],
                     op0=ALU.subtract,
                     op1=ALU.mult,
                 )
 
-        def mask_and_flip(u, f):
+        def mask(u, f):
             if is_unit(u):
-                dpre = dpre_of[u]
+                both_halves = dpre_of[u][:, f, :, :, :].rearrange("p h n t -> p h (n t)")
                 nc.vector.tensor_tensor(
-                    out=dpre[:, f, :, :],
-                    in0=dpre[:, f, :, :],
-                    in1=won_of[u][:, f, :].unsqueeze(1).to_broadcast([P, HALVES, C]),
+                    out=both_halves,
+                    in0=both_halves,
+                    in1=won_flipped_of[u][:, f, :, :].rearrange("p n t -> p (n t)").unsqueeze(1).to_broadcast([P, HALVES, C]),
                     op=ALU.mult,
                 )
-                d_flip = flipped.tile([P, HALVES, PACK, P], BF16, tag="flip")
-                for h in range(HALVES):
-                    for t in range(PACK):
-                        nc.tensor.transpose(d_flip[:, h, t, :], dpre[:, f, h, t * P : (t + 1) * P], ident[:])
-                d_grouped = d_mid.tile([P, HALVES, P, PACK], BF16, align_bytes=64)
-                nc.scalar.copy(out=d_grouped[:], in_=d_flip[:].rearrange("p h t n -> p h n t"))
-                d_grouped_of[(u, f)] = d_grouped
 
         def quantise_branch(u, f):
             if is_unit(u):
@@ -218,7 +250,7 @@ def tile_stsindividuallayer_pb_v_kernel(tc, agg, W, b, pre, grad_out, out):
                 nc.vector.quantize_mx(
                     out=d_codes_of[u][:, both, :].rearrange("p h n -> p (h n)").bitcast(E5M2X4),
                     scales=d_scales_of[u][:, both, :].rearrange("p h n -> p (h n)"),
-                    in_=d_grouped_of[(u, f)][:].rearrange("p h n t -> p (h n t)"),
+                    in_=dpre_of[u][:, f, :, :, :].rearrange("p h n t -> p (h n t)"),
                 )
 
         def multiply(u):
@@ -242,38 +274,39 @@ def tile_stsindividuallayer_pb_v_kernel(tc, agg, W, b, pre, grad_out, out):
         load_pre(0)
         load_pre(1)
         nc.sync.dma_start(out=grad[:], in_=grad_out[0].rearrange("w (a p) c -> p (w a) c", p=P))
-        load_w(0, 0)
-        load_w(0, 1)
         load_pre(2)
-        load_w(0, 2)
         sigmoid(0)
+        for f in range(BRANCHES):
+            glu_of_branch(nc.vector, 0, f)
         for r in range(ROUNDS):
-            begun, shared, done = r, r - 1, r - 2
+            begun, shared, masked, multiplied = r, r - 1, r - 2, r - MULTIPLY_AFTER
+            load_pre(r + PRE_TILES)
+            load_w(r)
             sigmoid(begun + 1)
-            for s in w_passes_of_round(r):
-                flip_w(s)
-            glu_of_branch(begun, 0)
+            flip_sg(shared)
             count_two(shared)
-            glu_of_branch(begun, 1)
-            count_three(shared)
-            glu_of_branch(begun, 2)
-            line_of_count(shared)
             top_of_two(begun)
-            share_of_grad(shared)
+            count_three(shared)
+            mask(masked, 0)
+            line_of_count(shared)
             top_of_three(begun)
+            share_of_grad(shared)
+            flip_share(shared)
+            mask(masked, 1)
             share_times_top(shared)
-            winners(begun)
-            load_pre(begun + PRE_AHEAD)
-            if r == 0:
-                for f in range(BRANCHES):
-                    load_w(1, f)
-            lhs_half(shared)
-            quantise_branch(done, 0)
-            rhs_half(shared)
-            quantise_branch(done, 1)
-            quantise_branch(done, 2)
+            flip_share_times_top(shared)
+            mask(masked, 2)
             for f in range(BRANCHES):
-                mask_and_flip(shared, f)
-            for s in w_passes_of_round(r - 1):
+                quantise_branch(masked, f)
+            first_bank = (r - FIRST_W_ROUND) * W_BANKS_A_ROUND
+            for s in range((first_bank - W_BANKS_A_ROUND) // 2, first_bank // 2):
                 quantise_w(s)
-            multiply(done)
+            winners(begun)
+            flip_won(shared)
+            for k in range(first_bank, first_bank + W_BANKS_A_ROUND):
+                flip_w_bank(k)
+            glu_engine = nc.gpsimd if is_unit(shared) else nc.vector
+            for f in range(BRANCHES):
+                glu_of_branch(glu_engine, begun + 1, f)
+                products(shared, f)
+            multiply(multiplied)

@@ -27,8 +27,9 @@ PRE_TILES = 3
 W_BANKS = WINDOWS * PASSES * 2
 W_BANKS_A_ROUND = 6
 FIRST_W_ROUND = 2
-MULTIPLY_AFTER = 4
-ROUNDS = UNITS + MULTIPLY_AFTER
+FIRST_MULTIPLY_ROUND = 4
+WAITING_UNITS = 3
+ROUNDS = UNITS + 2
 
 FLOPS = 2 * WINDOWS * NODES * C * BRANCHES * 2 * C
 BYTES = WINDOWS * (BRANCHES * NODES * 2 * C * 4 + BRANCHES * C * 2 * C * 2 + NODES * C * 2 + NODES * C * 4)
@@ -52,7 +53,7 @@ def tile_stsindividuallayer_pb_v_kernel(tc, agg, W, b, pre, grad_out, out):
         single = stack.enter_context(tc.tile_pool(name="single", bufs=1))
         double = stack.enter_context(tc.tile_pool(name="double", bufs=2))
         w_mid = stack.enter_context(tc.tile_pool(name="w_mid", bufs=W_BANKS_A_ROUND))
-        mx = stack.enter_context(tc.tile_pool(name="mx", bufs=MULTIPLY_AFTER - 1))
+        mx = stack.enter_context(tc.tile_pool(name="mx", bufs=WAITING_UNITS))
         sg_banks = stack.enter_context(tc.psum_pool(name="sg_banks", bufs=BRANCHES))
         flipped = stack.enter_context(tc.psum_pool(name="flipped", bufs=4))
         sums = stack.enter_context(tc.psum_pool(name="sums", bufs=1))
@@ -278,8 +279,9 @@ def tile_stsindividuallayer_pb_v_kernel(tc, agg, W, b, pre, grad_out, out):
         sigmoid(0)
         for f in range(BRANCHES):
             glu_of_branch(nc.vector, 0, f)
+        waiting = []
         for r in range(ROUNDS):
-            begun, shared, masked, multiplied = r, r - 1, r - 2, r - MULTIPLY_AFTER
+            begun, shared, masked = r, r - 1, r - 2
             load_pre(r + PRE_TILES)
             load_w(r)
             sigmoid(begun + 1)
@@ -309,4 +311,10 @@ def tile_stsindividuallayer_pb_v_kernel(tc, agg, W, b, pre, grad_out, out):
             for f in range(BRANCHES):
                 glu_of_branch(glu_engine, begun + 1, f)
                 products(shared, f)
-            multiply(multiplied)
+            if is_unit(masked):
+                waiting.append(masked)
+            if r >= FIRST_MULTIPLY_ROUND:
+                now = waiting[: (1 if first_bank < W_BANKS else 2)]
+                waiting = waiting[len(now) :]
+                for u in now:
+                    multiply(u)

@@ -39,6 +39,14 @@ def is_unit(u):
     return 0 <= u < UNITS
 
 
+def sorted_read(channels):
+    return channels.rearrange("p (u q e) -> p u e q", u=2, e=2)
+
+
+def sorted_tile(channels):
+    return channels.rearrange("p (u e q) -> p u e q", u=2, e=2)
+
+
 def window_and_rows(u):
     return u // NODE_TILES, slice((u % NODE_TILES) * P, (u % NODE_TILES + 1) * P)
 
@@ -68,7 +76,7 @@ def tile_stsindividuallayer_pb_v_kernel(tc, agg, W, b, pre, grad_out, out):
         w_codes = keep.tile([P, WINDOWS * PASSES, C], U32, align_bytes=64)
         w_scales = keep.tile([P, WINDOWS * PASSES, C], U8, align_bytes=64)
         pre_of, w_of, w_grouped_of = {}, {}, {}
-        sg_of, glu_of, top_of, won_of = {}, {}, {}, {}
+        sg_of, grad_sorted_of, glu_of, top_of, won_of = {}, {}, {}, {}, {}
         count_of, line_of, share_of, minus_share_top_of = {}, {}, {}, {}
         sg_flipped_of, share_flipped_of, minus_share_top_flipped_of, won_flipped_of = {}, {}, {}, {}
         dpre_of, d_codes_of, d_scales_of = {}, {}, {}
@@ -95,14 +103,18 @@ def tile_stsindividuallayer_pb_v_kernel(tc, agg, W, b, pre, grad_out, out):
                 if pair == 0:
                     w_grouped = w_mid.tile([P, C, PACK], BF16, align_bytes=64)
                     w_grouped_of[s] = w_grouped
-                w_flip = flipped.tile([P, 2, PACK, P], BF16, tag="flip")
+                w_flip = flipped.tile([P, 2, 2, P], F32, tag="flip")
                 for a in range(2):
-                    for t in range(PACK):
-                        j0 = (s % HALVES) * C + t * P
-                        nc.tensor.transpose(w_flip[:, a, t, :], w_raw[:, 2 * pair + a, j0 : j0 + P], ident[:])
+                    words = w_raw[:, 2 * pair + a, :].bitcast(F32)
+                    for u in range(2):
+                        m0 = (s % HALVES) * (C // 2) + u * P
+                        nc.tensor.transpose(w_flip[:, a, u, :], words[:, m0 : m0 + P], ident_f32[:])
                 nc.scalar.copy(
-                    out=w_grouped_of[s][:, 2 * pair * P : (2 * pair + 2) * P, :].rearrange("p (a c) t -> p a c t", a=2),
-                    in_=w_flip[:].rearrange("p a t c -> p a c t"),
+                    out=w_grouped_of[s][:, 2 * pair * P : (2 * pair + 2) * P, :]
+                    .rearrange("p c t -> p (c t)")
+                    .bitcast(F32)
+                    .rearrange("p (a c u) -> p a c u", a=2, u=2),
+                    in_=w_flip[:].rearrange("p a u c -> p a c u"),
                 )
 
         def quantise_w(s):
@@ -117,15 +129,28 @@ def tile_stsindividuallayer_pb_v_kernel(tc, agg, W, b, pre, grad_out, out):
             if is_unit(u):
                 sg = sig.tile([P, BRANCHES, C], F32)
                 for f in range(BRANCHES):
-                    nc.scalar.activation(out=sg[:, f, :], in_=pre_of[u][:, f, C : 2 * C], func=ACT.Sigmoid)
+                    nc.scalar.activation(
+                        out=sorted_tile(sg[:, f, :]), in_=sorted_read(pre_of[u][:, f, C : 2 * C]), func=ACT.Sigmoid
+                    )
                 sg_of[u] = sg
+
+        def sort_grad(u):
+            if is_unit(u):
+                grad_sorted = double.tile([P, C], BF16)
+                nc.scalar.copy(out=sorted_tile(grad_sorted[:]), in_=sorted_read(grad[:, u, :]))
+                grad_sorted_of[u] = grad_sorted
 
         def glu_of_branch(engine, u, f):
             if is_unit(u):
                 if f == 0:
                     glu = single.tile([P, BRANCHES, C], F32)
                     glu_of[u] = glu
-                engine.tensor_tensor(out=glu_of[u][:, f, :], in0=pre_of[u][:, f, 0:C], in1=sg_of[u][:, f, :], op=ALU.mult)
+                engine.tensor_tensor(
+                    out=sorted_tile(glu_of[u][:, f, :]),
+                    in0=sorted_read(pre_of[u][:, f, 0:C]),
+                    in1=sorted_tile(sg_of[u][:, f, :]),
+                    op=ALU.mult,
+                )
 
         def top_of_two(u):
             if is_unit(u):
@@ -167,7 +192,7 @@ def tile_stsindividuallayer_pb_v_kernel(tc, agg, W, b, pre, grad_out, out):
             if is_unit(u):
                 share = single.tile([P, C], F32)
                 nc.vector.scalar_tensor_tensor(
-                    out=share[:], in0=line_of[u][:], scalar=1.0 / 3.0, in1=grad[:, u, :], op0=ALU.max, op1=ALU.mult
+                    out=share[:], in0=line_of[u][:], scalar=1.0 / 3.0, in1=grad_sorted_of[u][:], op0=ALU.max, op1=ALU.mult
                 )
                 share_of[u] = share
 
@@ -285,6 +310,7 @@ def tile_stsindividuallayer_pb_v_kernel(tc, agg, W, b, pre, grad_out, out):
             load_pre(r + PRE_TILES)
             load_w(r)
             sigmoid(begun + 1)
+            sort_grad(begun)
             flip_sg(shared)
             count_two(shared)
             top_of_two(begun)

@@ -39,14 +39,6 @@ def is_unit(u):
     return 0 <= u < UNITS
 
 
-def sorted_read(channels):
-    return channels.rearrange("p (u q e) -> p u e q", u=2, e=2)
-
-
-def sorted_tile(channels):
-    return channels.rearrange("p (u e q) -> p u e q", u=2, e=2)
-
-
 def window_and_rows(u):
     return u // NODE_TILES, slice((u % NODE_TILES) * P, (u % NODE_TILES + 1) * P)
 
@@ -76,7 +68,7 @@ def tile_stsindividuallayer_pb_v_kernel(tc, agg, W, b, pre, grad_out, out):
         w_codes = keep.tile([P, WINDOWS * PASSES, C], U32, align_bytes=64)
         w_scales = keep.tile([P, WINDOWS * PASSES, C], U8, align_bytes=64)
         pre_of, w_of, w_grouped_of = {}, {}, {}
-        sg_of, grad_sorted_of, glu_of, top_of, won_of = {}, {}, {}, {}, {}
+        sg_of, glu_of, top_of, won_of = {}, {}, {}, {}
         count_of, line_of, share_of, minus_share_top_of = {}, {}, {}, {}
         sg_flipped_of, share_flipped_of, minus_share_top_flipped_of, won_flipped_of = {}, {}, {}, {}
         dpre_of, d_codes_of, d_scales_of = {}, {}, {}
@@ -103,18 +95,14 @@ def tile_stsindividuallayer_pb_v_kernel(tc, agg, W, b, pre, grad_out, out):
                 if pair == 0:
                     w_grouped = w_mid.tile([P, C, PACK], BF16, align_bytes=64)
                     w_grouped_of[s] = w_grouped
-                w_flip = flipped.tile([P, 2, 2, P], F32, tag="flip")
+                w_flip = flipped.tile([P, 2, PACK, P], BF16, tag="flip")
                 for a in range(2):
-                    words = w_raw[:, 2 * pair + a, :].bitcast(F32)
-                    for u in range(2):
-                        m0 = (s % HALVES) * (C // 2) + u * P
-                        nc.tensor.transpose(w_flip[:, a, u, :], words[:, m0 : m0 + P], ident_f32[:])
+                    for t in range(PACK):
+                        j0 = (s % HALVES) * C + t * P
+                        nc.tensor.transpose(w_flip[:, a, t, :], w_raw[:, 2 * pair + a, j0 : j0 + P], ident[:])
                 nc.scalar.copy(
-                    out=w_grouped_of[s][:, 2 * pair * P : (2 * pair + 2) * P, :]
-                    .rearrange("p c t -> p (c t)")
-                    .bitcast(F32)
-                    .rearrange("p (a c u) -> p a c u", a=2, u=2),
-                    in_=w_flip[:].rearrange("p a u c -> p a c u"),
+                    out=w_grouped_of[s][:, 2 * pair * P : (2 * pair + 2) * P, :].rearrange("p (a c) t -> p a c t", a=2),
+                    in_=w_flip[:].rearrange("p a t c -> p a c t"),
                 )
 
         def quantise_w(s):
@@ -129,27 +117,17 @@ def tile_stsindividuallayer_pb_v_kernel(tc, agg, W, b, pre, grad_out, out):
             if is_unit(u):
                 sg = sig.tile([P, BRANCHES, C], F32)
                 for f in range(BRANCHES):
-                    nc.scalar.activation(
-                        out=sorted_tile(sg[:, f, :]), in_=sorted_read(pre_of[u][:, f, C : 2 * C]), func=ACT.Sigmoid
-                    )
+                    nc.scalar.activation(out=sg[:, f, :], in_=pre_of[u][:, f, C : 2 * C], func=ACT.Sigmoid)
                 sg_of[u] = sg
 
-        def sort_grad(u):
+        def glu_of_branches(engine, u, first, last):
             if is_unit(u):
-                grad_sorted = double.tile([P, C], BF16)
-                nc.scalar.copy(out=sorted_tile(grad_sorted[:]), in_=sorted_read(grad[:, u, :]))
-                grad_sorted_of[u] = grad_sorted
-
-        def glu_of_branch(engine, u, f):
-            if is_unit(u):
-                if f == 0:
+                if first == 0:
                     glu = single.tile([P, BRANCHES, C], F32)
                     glu_of[u] = glu
+                branches = slice(first, last + 1)
                 engine.tensor_tensor(
-                    out=sorted_tile(glu_of[u][:, f, :]),
-                    in0=sorted_read(pre_of[u][:, f, 0:C]),
-                    in1=sorted_tile(sg_of[u][:, f, :]),
-                    op=ALU.mult,
+                    out=glu_of[u][:, branches, :], in0=pre_of[u][:, branches, 0:C], in1=sg_of[u][:, branches, :], op=ALU.mult
                 )
 
         def top_of_two(u):
@@ -192,7 +170,7 @@ def tile_stsindividuallayer_pb_v_kernel(tc, agg, W, b, pre, grad_out, out):
             if is_unit(u):
                 share = single.tile([P, C], F32)
                 nc.vector.scalar_tensor_tensor(
-                    out=share[:], in0=line_of[u][:], scalar=1.0 / 3.0, in1=grad_sorted_of[u][:], op0=ALU.max, op1=ALU.mult
+                    out=share[:], in0=line_of[u][:], scalar=1.0 / 3.0, in1=grad[:, u, :], op0=ALU.max, op1=ALU.mult
                 )
                 share_of[u] = share
 
@@ -303,14 +281,13 @@ def tile_stsindividuallayer_pb_v_kernel(tc, agg, W, b, pre, grad_out, out):
         load_pre(2)
         sigmoid(0)
         for f in range(BRANCHES):
-            glu_of_branch(nc.vector, 0, f)
+            glu_of_branches(nc.vector, 0, f, f)
         waiting = []
         for r in range(ROUNDS):
             begun, shared, masked = r, r - 1, r - 2
             load_pre(r + PRE_TILES)
             load_w(r)
             sigmoid(begun + 1)
-            sort_grad(begun)
             flip_sg(shared)
             count_two(shared)
             top_of_two(begun)
@@ -323,9 +300,10 @@ def tile_stsindividuallayer_pb_v_kernel(tc, agg, W, b, pre, grad_out, out):
             mask(masked, 1)
             share_times_top(shared)
             flip_share_times_top(shared)
+            quantise_branch(masked, 0)
             mask(masked, 2)
-            for f in range(BRANCHES):
-                quantise_branch(masked, f)
+            quantise_branch(masked, 1)
+            quantise_branch(masked, 2)
             first_bank = (r - FIRST_W_ROUND) * W_BANKS_A_ROUND
             for s in range((first_bank - W_BANKS_A_ROUND) // 2, first_bank // 2):
                 quantise_w(s)
@@ -333,10 +311,13 @@ def tile_stsindividuallayer_pb_v_kernel(tc, agg, W, b, pre, grad_out, out):
             flip_won(shared)
             for k in range(first_bank, first_bank + W_BANKS_A_ROUND):
                 flip_w_bank(k)
-            glu_engine = nc.gpsimd if is_unit(shared) else nc.vector
-            for f in range(BRANCHES):
-                glu_of_branch(glu_engine, begun + 1, f)
-                products(shared, f)
+            if is_unit(shared):
+                glu_of_branches(nc.gpsimd, begun + 1, 0, BRANCHES - 1)
+                for f in range(BRANCHES):
+                    products(shared, f)
+            else:
+                for f in range(BRANCHES):
+                    glu_of_branches(nc.vector, begun + 1, f, f)
             if is_unit(masked):
                 waiting.append(masked)
             if r >= FIRST_MULTIPLY_ROUND:

@@ -25,11 +25,11 @@ CH_TILES = C // P
 UNITS = WINDOWS * NODE_TILES
 PRE_TILES = 3
 W_BANKS = WINDOWS * PASSES * 2
-W_BANKS_A_ROUND = 6
+W_BANKS_A_ROUND = 4
 FIRST_W_ROUND = 2
-FIRST_MULTIPLY_ROUND = 4
-WAITING_UNITS = 3
-ROUNDS = UNITS + 2
+FIRST_MULTIPLY_ROUND = 5
+WAITING_UNITS = 4
+ROUNDS = UNITS + 3
 
 FLOPS = 2 * WINDOWS * NODES * C * BRANCHES * 2 * C
 BYTES = WINDOWS * (BRANCHES * NODES * 2 * C * 4 + BRANCHES * C * 2 * C * 2 + NODES * C * 2 + NODES * C * 4)
@@ -48,10 +48,11 @@ def tile_stsindividuallayer_pb_v_kernel(tc, agg, W, b, pre, grad_out, out):
     with ExitStack() as stack:
         keep = stack.enter_context(tc.tile_pool(name="keep", bufs=1))
         pre_in = stack.enter_context(tc.tile_pool(name="pre_in", bufs=PRE_TILES))
-        w_in = stack.enter_context(tc.tile_pool(name="w_in", bufs=WINDOWS * BRANCHES))
-        sig = stack.enter_context(tc.tile_pool(name="sig", bufs=3))
+        w_in = stack.enter_context(tc.tile_pool(name="w_in", bufs=4))
+        sig = stack.enter_context(tc.tile_pool(name="sig", bufs=4))
         single = stack.enter_context(tc.tile_pool(name="single", bufs=1))
         double = stack.enter_context(tc.tile_pool(name="double", bufs=2))
+        triple = stack.enter_context(tc.tile_pool(name="triple", bufs=3))
         w_mid = stack.enter_context(tc.tile_pool(name="w_mid", bufs=W_BANKS_A_ROUND))
         mx = stack.enter_context(tc.tile_pool(name="mx", bufs=WAITING_UNITS))
         sg_banks = stack.enter_context(tc.psum_pool(name="sg_banks", bufs=BRANCHES))
@@ -68,9 +69,9 @@ def tile_stsindividuallayer_pb_v_kernel(tc, agg, W, b, pre, grad_out, out):
         w_codes = keep.tile([P, WINDOWS * PASSES, C], U32, align_bytes=64)
         w_scales = keep.tile([P, WINDOWS * PASSES, C], U8, align_bytes=64)
         pre_of, w_of, w_grouped_of = {}, {}, {}
-        sg_of, glu_of, top_of, won_of = {}, {}, {}, {}
-        count_of, line_of, share_of, minus_share_top_of = {}, {}, {}, {}
-        sg_flipped_of, share_flipped_of, minus_share_top_flipped_of, won_flipped_of = {}, {}, {}, {}
+        sg_of, glu_of, top_of, minus_of, lost_of = {}, {}, {}, {}, {}
+        losers_of, half_grad_of, share_of, minus_share_top_of = {}, {}, {}, {}
+        sg_flipped_of, minus_flipped_of, won_of = {}, {}, {}
         dpre_of, d_codes_of, d_scales_of = {}, {}, {}
 
         def load_pre(u):
@@ -81,12 +82,10 @@ def tile_stsindividuallayer_pb_v_kernel(tc, agg, W, b, pre, grad_out, out):
                     nc.sync.dma_start(out=pre_t[:, f, :], in_=pre[0, w, f, rows, :])
                 pre_of[u] = pre_t
 
-        def load_w(w):
-            if w < WINDOWS:
-                for f in range(BRANCHES):
-                    w_raw = w_in.tile([P, CH_TILES, 2 * C], BF16)
-                    nc.sync.dma_start(out=w_raw[:], in_=W[w, f].rearrange("(a p) j -> p a j", p=P))
-                    w_of[(w, f)] = w_raw
+        def load_w(i):
+            w_raw = w_in.tile([P, CH_TILES, 2 * C], BF16)
+            nc.sync.dma_start(out=w_raw[:], in_=W[i // BRANCHES, i % BRANCHES].rearrange("(a p) j -> p a j", p=P))
+            w_of[(i // BRANCHES, i % BRANCHES)] = w_raw
 
         def flip_w_bank(k):
             if 0 <= k < W_BANKS:
@@ -123,7 +122,7 @@ def tile_stsindividuallayer_pb_v_kernel(tc, agg, W, b, pre, grad_out, out):
         def glu_of_branches(engine, u, first, last):
             if is_unit(u):
                 if first == 0:
-                    glu = single.tile([P, BRANCHES, C], F32)
+                    glu = double.tile([P, BRANCHES, C], F32)
                     glu_of[u] = glu
                 branches = slice(first, last + 1)
                 engine.tensor_tensor(
@@ -140,47 +139,11 @@ def tile_stsindividuallayer_pb_v_kernel(tc, agg, W, b, pre, grad_out, out):
             if is_unit(u):
                 nc.vector.tensor_tensor(out=top_of[u][:], in0=top_of[u][:], in1=glu_of[u][:, 2, :], op=ALU.max)
 
-        def winners(u):
+        def minus_top(u):
             if is_unit(u):
-                won = double.tile([P, BRANCHES, C], BF16)
-                nc.vector.tensor_tensor(
-                    out=won[:], in0=glu_of[u][:], in1=top_of[u][:].unsqueeze(1).to_broadcast([P, BRANCHES, C]), op=ALU.is_equal
-                )
-                won_of[u] = won
-
-        def count_two(u):
-            if is_unit(u):
-                count = single.tile([P, C], BF16)
-                nc.vector.tensor_tensor(out=count[:], in0=won_of[u][:, 0, :], in1=won_of[u][:, 1, :], op=ALU.add)
-                count_of[u] = count
-
-        def count_three(u):
-            if is_unit(u):
-                nc.vector.tensor_tensor(out=count_of[u][:], in0=count_of[u][:], in1=won_of[u][:, 2, :], op=ALU.add)
-
-        def line_of_count(u):
-            if is_unit(u):
-                line = single.tile([P, C], BF16)
-                nc.vector.tensor_scalar(
-                    out=line[:], in0=count_of[u][:], scalar1=-0.5, scalar2=1.5, op0=ALU.mult, op1=ALU.add
-                )
-                line_of[u] = line
-
-        def share_of_grad(u):
-            if is_unit(u):
-                share = single.tile([P, C], F32)
-                nc.vector.scalar_tensor_tensor(
-                    out=share[:], in0=line_of[u][:], scalar=1.0 / 3.0, in1=grad[:, u, :], op0=ALU.max, op1=ALU.mult
-                )
-                share_of[u] = share
-
-        def share_times_top(u):
-            if is_unit(u):
-                minus_share_top = single.tile([P, C], F32)
-                nc.vector.scalar_tensor_tensor(
-                    out=minus_share_top[:], in0=share_of[u][:], scalar=-1.0, in1=top_of[u][:], op0=ALU.mult, op1=ALU.mult
-                )
-                minus_share_top_of[u] = minus_share_top
+                minus = double.tile([P, C], F32)
+                nc.gpsimd.tensor_scalar(out=minus[:], in0=top_of[u][:], scalar1=-1.0, scalar2=0.0, op0=ALU.mult, op1=ALU.add)
+                minus_of[u] = minus
 
         def flip_sg(u):
             if is_unit(u):
@@ -190,33 +153,65 @@ def tile_stsindividuallayer_pb_v_kernel(tc, agg, W, b, pre, grad_out, out):
                         nc.tensor.transpose(sg_flipped[:, t, :], sg_of[u][:, f, t * P : (t + 1) * P], ident_f32[:])
                     sg_flipped_of[(u, f)] = sg_flipped
 
-        def flip_plane(plane, regrouped):
-            bank = flipped.tile([P, PACK, P], F32, tag="flip")
-            for t in range(PACK):
-                nc.tensor.transpose(bank[:, t, :], plane[:, t * P : (t + 1) * P], ident_f32[:])
-            nc.scalar.copy(out=regrouped[:], in_=bank[:].rearrange("p t n -> p n t"))
-
-        def flip_share(u):
+        def flip_gap(u, f):
             if is_unit(u):
-                share_flipped = single.tile([P, P, PACK], F32)
-                flip_plane(share_of[u], share_flipped)
-                share_flipped_of[u] = share_flipped
+                if f == 0:
+                    lost = double.tile([P, BRANCHES, P, PACK], BF16)
+                    lost_of[u] = lost
+                bank = flipped.tile([P, PACK, P], F32, tag="flip")
+                for t in range(PACK):
+                    cols = slice(t * P, (t + 1) * P)
+                    nc.tensor.matmul(bank[:, t, :], lhsT=glu_of[u][:, f, cols], rhs=ident_f32[:], is_transpose=True, start=True, stop=False)
+                    nc.tensor.matmul(bank[:, t, :], lhsT=minus_of[u][:, cols], rhs=ident_f32[:], is_transpose=True, start=False, stop=True)
+                nc.scalar.activation(out=lost_of[u][:, f, :, :], in_=bank[:].rearrange("p t n -> p n t"), func=ACT.Sign)
 
-        def flip_share_times_top(u):
+        def winners(u):
             if is_unit(u):
-                minus_share_top_flipped = single.tile([P, P, PACK], F32)
-                flip_plane(minus_share_top_of[u], minus_share_top_flipped)
-                minus_share_top_flipped_of[u] = minus_share_top_flipped
+                won = triple.tile([P, BRANCHES, P, PACK], BF16)
+                nc.scalar.activation(out=won[:], in_=lost_of[u][:], func=ACT.Copy, bias=1.0)
+                won_of[u] = won
 
-        def flip_won(u):
+        def flip_minus_top(u):
             if is_unit(u):
-                won_flipped = double.tile([P, BRANCHES, P, PACK], BF16)
-                for f in range(BRANCHES):
-                    bank = flipped.tile([P, PACK, P], BF16, tag="flip")
-                    for t in range(PACK):
-                        nc.tensor.transpose(bank[:, t, :], won_of[u][:, f, t * P : (t + 1) * P], ident[:])
-                    nc.scalar.copy(out=won_flipped[:, f, :, :], in_=bank[:].rearrange("p t n -> p n t"))
-                won_flipped_of[u] = won_flipped
+                bank = flipped.tile([P, PACK, P], F32, tag="flip")
+                for t in range(PACK):
+                    nc.tensor.transpose(bank[:, t, :], minus_of[u][:, t * P : (t + 1) * P], ident_f32[:])
+                minus_flipped_of[u] = bank
+
+        def flip_grad(u):
+            if is_unit(u):
+                bank = flipped.tile([P, PACK, P], BF16, tag="flip")
+                for t in range(PACK):
+                    nc.tensor.transpose(bank[:, t, :], grad[:, u, t * P : (t + 1) * P], ident[:])
+                half_grad = double.tile([P, P, PACK], F32)
+                nc.scalar.activation(out=half_grad[:], in_=bank[:].rearrange("p t n -> p n t"), func=ACT.Copy, scale=-0.5)
+                half_grad_of[u] = half_grad
+
+        def lost_two(u):
+            if is_unit(u):
+                losers = single.tile([P, P, PACK], BF16)
+                nc.vector.tensor_tensor(out=losers[:], in0=lost_of[u][:, 0, :, :], in1=lost_of[u][:, 1, :, :], op=ALU.add)
+                losers_of[u] = losers
+
+        def lost_three(u):
+            if is_unit(u):
+                nc.vector.tensor_tensor(out=losers_of[u][:], in0=losers_of[u][:], in1=lost_of[u][:, 2, :, :], op=ALU.add)
+
+        def share_of_grad(u):
+            if is_unit(u):
+                share = single.tile([P, P, PACK], F32)
+                nc.vector.scalar_tensor_tensor(
+                    out=share[:], in0=losers_of[u][:], scalar=-2.0 / 3.0, in1=half_grad_of[u][:], op0=ALU.min, op1=ALU.mult
+                )
+                share_of[u] = share
+
+        def share_times_top(u):
+            if is_unit(u):
+                minus_share_top = single.tile([P, P, PACK], F32)
+                nc.vector.tensor_tensor(
+                    out=minus_share_top[:], in0=minus_flipped_of[u][:].rearrange("p t n -> p n t"), in1=share_of[u][:], op=ALU.mult
+                )
+                minus_share_top_of[u] = minus_share_top
 
         def products(u, f):
             if is_unit(u):
@@ -224,12 +219,12 @@ def tile_stsindividuallayer_pb_v_kernel(tc, agg, W, b, pre, grad_out, out):
                     dpre = single.tile([P, BRANCHES, HALVES, P, PACK], BF16, align_bytes=64)
                     dpre_of[u] = dpre
                 sg_by_node = sg_flipped_of[(u, f)][:].rearrange("p t n -> p n t")
-                nc.vector.tensor_tensor(out=dpre_of[u][:, f, 0, :, :], in0=sg_by_node, in1=share_flipped_of[u][:], op=ALU.mult)
+                nc.vector.tensor_tensor(out=dpre_of[u][:, f, 0, :, :], in0=sg_by_node, in1=share_of[u][:], op=ALU.mult)
                 nc.vector.scalar_tensor_tensor(
                     out=dpre_of[u][:, f, 1, :, :],
                     in0=sg_by_node,
                     scalar=1.0,
-                    in1=minus_share_top_flipped_of[u][:],
+                    in1=minus_share_top_of[u][:],
                     op0=ALU.subtract,
                     op1=ALU.mult,
                 )
@@ -240,7 +235,7 @@ def tile_stsindividuallayer_pb_v_kernel(tc, agg, W, b, pre, grad_out, out):
                 nc.vector.tensor_tensor(
                     out=both_halves,
                     in0=both_halves,
-                    in1=won_flipped_of[u][:, f, :, :].rearrange("p n t -> p (n t)").unsqueeze(1).to_broadcast([P, HALVES, C]),
+                    in1=won_of[u][:, f, :, :].rearrange("p n t -> p (n t)").unsqueeze(1).to_broadcast([P, HALVES, C]),
                     op=ALU.mult,
                 )
 
@@ -282,46 +277,44 @@ def tile_stsindividuallayer_pb_v_kernel(tc, agg, W, b, pre, grad_out, out):
         sigmoid(0)
         for f in range(BRANCHES):
             glu_of_branches(nc.vector, 0, f, f)
-        waiting = []
+        w_loads = {0: [0, 1, 2], 1: [3], 3: [4], 4: [5]}
+        multiplies = {5: [0], 6: [1], 7: [2], 8: [3, 4], 9: [5, 6], 10: [7]}
         for r in range(ROUNDS):
-            begun, shared, masked = r, r - 1, r - 2
+            begun, gapped, shared, masked = r, r - 1, r - 2, r - 3
             load_pre(r + PRE_TILES)
-            load_w(r)
+            for i in w_loads.get(r, []):
+                load_w(i)
             sigmoid(begun + 1)
             flip_sg(shared)
-            count_two(shared)
+            flip_minus_top(shared)
+            for f in range(BRANCHES):
+                flip_gap(gapped, f)
+            lost_two(shared)
             top_of_two(begun)
-            count_three(shared)
+            lost_three(shared)
             mask(masked, 0)
-            line_of_count(shared)
-            top_of_three(begun)
             share_of_grad(shared)
-            flip_share(shared)
             mask(masked, 1)
-            share_times_top(shared)
-            flip_share_times_top(shared)
             quantise_branch(masked, 0)
             mask(masked, 2)
             quantise_branch(masked, 1)
-            quantise_branch(masked, 2)
             first_bank = (r - FIRST_W_ROUND) * W_BANKS_A_ROUND
-            for s in range((first_bank - W_BANKS_A_ROUND) // 2, first_bank // 2):
-                quantise_w(s)
-            winners(begun)
-            flip_won(shared)
-            for k in range(first_bank, first_bank + W_BANKS_A_ROUND):
-                flip_w_bank(k)
+            quantise_w((first_bank - W_BANKS_A_ROUND) // 2)
+            quantise_branch(masked, 2)
+            quantise_w((first_bank - W_BANKS_A_ROUND) // 2 + 1)
+            top_of_three(begun)
+            minus_top(begun)
             if is_unit(shared):
                 glu_of_branches(nc.gpsimd, begun + 1, 0, BRANCHES - 1)
+                share_times_top(shared)
                 for f in range(BRANCHES):
                     products(shared, f)
             else:
                 for f in range(BRANCHES):
                     glu_of_branches(nc.vector, begun + 1, f, f)
-            if is_unit(masked):
-                waiting.append(masked)
-            if r >= FIRST_MULTIPLY_ROUND:
-                now = waiting[: (1 if first_bank < W_BANKS else 2)]
-                waiting = waiting[len(now) :]
-                for u in now:
-                    multiply(u)
+            winners(gapped)
+            for u in multiplies.get(r, []):
+                multiply(u)
+            for k in range(first_bank, first_bank + W_BANKS_A_ROUND):
+                flip_w_bank(k)
+            flip_grad(gapped)

@@ -92,16 +92,17 @@ def tile_stsindividuallayer_pb_v_kernel(tc, agg, W, b, pre, grad_out, out):
                 s, pair = k // 2, k % 2
                 w_raw = w_of[(s // PASSES, (s % PASSES) // HALVES)]
                 if pair == 0:
-                    w_grouped = w_mid.tile([P, C, PACK], BF16, align_bytes=64)
+                    w_grouped = w_mid.tile([P, C, 2], F32, align_bytes=64)
                     w_grouped_of[s] = w_grouped
-                w_flip = flipped.tile([P, 2, PACK, P], BF16, tag="flip")
+                w_flip = flipped.tile([P, 2, 2, P], F32, tag="flip")
                 for a in range(2):
-                    for t in range(PACK):
-                        j0 = (s % HALVES) * C + t * P
-                        nc.tensor.transpose(w_flip[:, a, t, :], w_raw[:, 2 * pair + a, j0 : j0 + P], ident[:])
+                    words = w_raw[:, 2 * pair + a, :].bitcast(F32)
+                    for v in range(2):
+                        w0 = (s % HALVES) * (C // 2) + v * P
+                        nc.tensor.transpose(w_flip[:, a, v, :], words[:, w0 : w0 + P], ident_f32[:])
                 nc.scalar.copy(
-                    out=w_grouped_of[s][:, 2 * pair * P : (2 * pair + 2) * P, :].rearrange("p (a c) t -> p a c t", a=2),
-                    in_=w_flip[:].rearrange("p a t c -> p a c t"),
+                    out=w_grouped_of[s][:, 2 * pair * P : (2 * pair + 2) * P, :].rearrange("p (a c) v -> p a c v", a=2),
+                    in_=w_flip[:].rearrange("p a v c -> p a c v"),
                 )
 
         def quantise_w(s):
@@ -109,14 +110,20 @@ def tile_stsindividuallayer_pb_v_kernel(tc, agg, W, b, pre, grad_out, out):
                 nc.vector.quantize_mx(
                     out=w_codes[:, s, :].bitcast(E4M3X4),
                     scales=w_scales[:, s, :],
-                    in_=w_grouped_of[s][:].rearrange("p c t -> p (c t)"),
+                    in_=w_grouped_of[s][:].rearrange("p c v -> p (c v)").bitcast(BF16),
                 )
+
+        def by_parity(channels):
+            return channels.rearrange("p (v q e) -> p v e q", v=2, e=2)
+
+        def in_blocks(channels):
+            return channels.rearrange("p (v e q) -> p v e q", v=2, e=2)
 
         def sigmoid(u):
             if is_unit(u):
                 sg = sig.tile([P, BRANCHES, C], F32)
                 for f in range(BRANCHES):
-                    nc.scalar.activation(out=sg[:, f, :], in_=pre_of[u][:, f, C : 2 * C], func=ACT.Sigmoid)
+                    nc.scalar.activation(out=in_blocks(sg[:, f, :]), in_=by_parity(pre_of[u][:, f, C : 2 * C]), func=ACT.Sigmoid)
                 sg_of[u] = sg
 
         def glu_of_branches(engine, u, first, last):
@@ -124,10 +131,10 @@ def tile_stsindividuallayer_pb_v_kernel(tc, agg, W, b, pre, grad_out, out):
                 if first == 0:
                     glu = double.tile([P, BRANCHES, C], F32)
                     glu_of[u] = glu
-                branches = slice(first, last + 1)
-                engine.tensor_tensor(
-                    out=glu_of[u][:, branches, :], in0=pre_of[u][:, branches, 0:C], in1=sg_of[u][:, branches, :], op=ALU.mult
-                )
+                for f in range(first, last + 1):
+                    engine.tensor_tensor(
+                        out=in_blocks(glu_of[u][:, f, :]), in0=by_parity(pre_of[u][:, f, 0:C]), in1=in_blocks(sg_of[u][:, f, :]), op=ALU.mult
+                    )
 
         def top_of_two(u):
             if is_unit(u):
@@ -180,11 +187,17 @@ def tile_stsindividuallayer_pb_v_kernel(tc, agg, W, b, pre, grad_out, out):
 
         def flip_grad(u):
             if is_unit(u):
-                bank = flipped.tile([P, PACK, P], BF16, tag="flip")
-                for t in range(PACK):
-                    nc.tensor.transpose(bank[:, t, :], grad[:, u, t * P : (t + 1) * P], ident[:])
+                bank = flipped.tile([P, 2, P], F32, tag="flip")
+                words = grad[:, u, :].bitcast(F32)
+                for v in range(2):
+                    nc.tensor.transpose(bank[:, v, :], words[:, v * P : (v + 1) * P], ident_f32[:])
                 half_grad = double.tile([P, P, PACK], F32)
-                nc.scalar.activation(out=half_grad[:], in_=bank[:].rearrange("p t n -> p n t"), func=ACT.Copy, scale=-0.5)
+                nc.scalar.activation(
+                    out=half_grad[:].rearrange("p n (v e) -> p n v e", v=2),
+                    in_=bank[:].rearrange("p v n -> p (v n)").bitcast(BF16).rearrange("p (v n e) -> p n v e", v=2, e=2),
+                    func=ACT.Copy,
+                    scale=-0.5,
+                )
                 half_grad_of[u] = half_grad
 
         def lost_two(u):

@@ -63,7 +63,6 @@ def tile_stsindividuallayer_pb_v_kernel(tc, agg, W, b, pre, grad_out, out):
         make_identity(nc, ident[:])
         ident_f32 = keep.tile([P, P], F32)
         make_identity(nc, ident_f32[:])
-        stack.enter_context(tc.manual_schedule())
 
         grad = keep.tile([P, UNITS, C], BF16)
         w_codes = keep.tile([P, WINDOWS * PASSES, C], U32, align_bytes=64)

@@ -78,7 +78,11 @@ def tile_stsindividuallayer_pb_v_kernel(tc, agg, W, b, pre, grad_out, out):
                 w, rows = window_and_rows(u)
                 pre_t = pre_in.tile([P, BRANCHES, 2 * C], F32)
                 for f in range(BRANCHES):
-                    nc.sync.dma_start(out=pre_t[:, f, :], in_=pre[0, w, f, rows, :])
+                    if u == 0:
+                        nc.sync.dma_start(out=pre_t[:, f, C : 2 * C], in_=pre[0, w, f, rows, C : 2 * C])
+                        nc.sync.dma_start(out=pre_t[:, f, 0:C], in_=pre[0, w, f, rows, 0:C])
+                    else:
+                        nc.sync.dma_start(out=pre_t[:, f, :], in_=pre[0, w, f, rows, :])
                 pre_of[u] = pre_t
 
         def load_w(i):
@@ -148,7 +152,7 @@ def tile_stsindividuallayer_pb_v_kernel(tc, agg, W, b, pre, grad_out, out):
         def minus_top(u):
             if is_unit(u):
                 minus = double.tile([P, C], F32)
-                nc.gpsimd.tensor_scalar(out=minus[:], in0=top_of[u][:], scalar1=-1.0, scalar2=0.0, op0=ALU.mult, op1=ALU.add)
+                nc.scalar.activation(out=minus[:], in_=top_of[u][:], func=ACT.Copy, scale=-1.0)
                 minus_of[u] = minus
 
         def flip_sg(u):
@@ -318,12 +322,12 @@ def tile_stsindividuallayer_pb_v_kernel(tc, agg, W, b, pre, grad_out, out):
             minus_top(begun)
             if is_unit(shared):
                 glu_of_branches(nc.gpsimd, begun + 1, 0, BRANCHES - 1)
-                share_times_top(shared)
-                for f in range(BRANCHES):
-                    products(shared, f)
             else:
                 for f in range(BRANCHES):
                     glu_of_branches(nc.vector, begun + 1, f, f)
+            share_times_top(shared)
+            for f in range(BRANCHES):
+                products(shared, f)
             winners(gapped)
             for u in multiplies.get(r, []):
                 multiply(u)

@@ -14,6 +14,7 @@ ACT = mybir.ActivationFunctionType
 
 P = 128
 PACK = 4
+PAIR = 2
 WINDOWS = 2
 BRANCHES = 3
 NODES = 512
@@ -24,10 +25,11 @@ NODE_TILES = NODES // P
 CH_TILES = C // P
 UNITS = WINDOWS * NODE_TILES
 PRE_TILES = 3
-W_BANKS = WINDOWS * PASSES * 2
-W_BANKS_A_ROUND = 4
+VECTOR_GLU_UNITS = 3
+W_TILES = WINDOWS * BRANCHES
+W_BUFFERS = 4
+W_BANKS_A_TILE = 4
 FIRST_W_ROUND = 2
-FIRST_MULTIPLY_ROUND = 5
 WAITING_UNITS = 4
 ROUNDS = UNITS + 3
 
@@ -43,34 +45,40 @@ def window_and_rows(u):
     return u // NODE_TILES, slice((u % NODE_TILES) * P, (u % NODE_TILES + 1) * P)
 
 
+def as_in_dram(channels):
+    return channels.rearrange("p (v q e) -> p v e q", v=PAIR, e=PAIR)
+
+
+def in_blocks(channels):
+    return channels.rearrange("p (v e q) -> p v e q", v=PAIR, e=PAIR)
+
+
 def tile_stsindividuallayer_pb_v_kernel(tc, agg, W, b, pre, grad_out, out):
     nc = tc.nc
     with ExitStack() as stack:
         keep = stack.enter_context(tc.tile_pool(name="keep", bufs=1))
         pre_in = stack.enter_context(tc.tile_pool(name="pre_in", bufs=PRE_TILES))
-        w_in = stack.enter_context(tc.tile_pool(name="w_in", bufs=4))
+        w_in = stack.enter_context(tc.tile_pool(name="w_in", bufs=W_BUFFERS))
         sig = stack.enter_context(tc.tile_pool(name="sig", bufs=4))
         single = stack.enter_context(tc.tile_pool(name="single", bufs=1))
         double = stack.enter_context(tc.tile_pool(name="double", bufs=2))
         triple = stack.enter_context(tc.tile_pool(name="triple", bufs=3))
-        w_mid = stack.enter_context(tc.tile_pool(name="w_mid", bufs=W_BANKS_A_ROUND))
+        w_mid = stack.enter_context(tc.tile_pool(name="w_mid", bufs=2 * HALVES))
         mx = stack.enter_context(tc.tile_pool(name="mx", bufs=WAITING_UNITS))
         sg_banks = stack.enter_context(tc.psum_pool(name="sg_banks", bufs=BRANCHES))
         flipped = stack.enter_context(tc.psum_pool(name="flipped", bufs=4))
         sums = stack.enter_context(tc.psum_pool(name="sums", bufs=1))
 
-        ident = keep.tile([P, P], BF16)
+        ident = keep.tile([P, P], F32)
         make_identity(nc, ident[:])
-        ident_f32 = keep.tile([P, P], F32)
-        make_identity(nc, ident_f32[:])
 
         grad = keep.tile([P, UNITS, C], BF16)
         w_codes = keep.tile([P, WINDOWS * PASSES, C], U32, align_bytes=64)
         w_scales = keep.tile([P, WINDOWS * PASSES, C], U8, align_bytes=64)
         pre_of, w_of, w_grouped_of = {}, {}, {}
-        sg_of, glu_of, top_of, minus_of, lost_of = {}, {}, {}, {}, {}
+        sg_of, glu_of, top_of, minus_top_of = {}, {}, {}, {}
+        sg_flipped_of, minus_top_flipped_of, lost_of, won_of = {}, {}, {}, {}
         losers_of, half_grad_of, share_of, minus_share_top_of = {}, {}, {}, {}
-        sg_flipped_of, minus_flipped_of, won_of = {}, {}, {}
         dpre_of, d_codes_of, d_scales_of = {}, {}, {}
 
         def load_pre(u):
@@ -88,56 +96,50 @@ def tile_stsindividuallayer_pb_v_kernel(tc, agg, W, b, pre, grad_out, out):
         def load_w(i):
             w_raw = w_in.tile([P, CH_TILES, 2 * C], BF16)
             nc.sync.dma_start(out=w_raw[:], in_=W[i // BRANCHES, i % BRANCHES].rearrange("(a p) j -> p a j", p=P))
-            w_of[(i // BRANCHES, i % BRANCHES)] = w_raw
+            w_of[i] = w_raw
 
-        def flip_w_bank(k):
-            if 0 <= k < W_BANKS:
-                s, pair = k // 2, k % 2
-                w_raw = w_of[(s // PASSES, (s % PASSES) // HALVES)]
-                if pair == 0:
-                    w_grouped = w_mid.tile([P, C, 2], F32, align_bytes=64)
-                    w_grouped_of[s] = w_grouped
-                w_flip = flipped.tile([P, 2, 2, P], F32, tag="flip")
-                for a in range(2):
-                    words = w_raw[:, 2 * pair + a, :].bitcast(F32)
-                    for v in range(2):
-                        w0 = (s % HALVES) * (C // 2) + v * P
-                        nc.tensor.transpose(w_flip[:, a, v, :], words[:, w0 : w0 + P], ident_f32[:])
-                nc.scalar.copy(
-                    out=w_grouped_of[s][:, 2 * pair * P : (2 * pair + 2) * P, :].rearrange("p (a c) v -> p a c v", a=2),
-                    in_=w_flip[:].rearrange("p a v c -> p a c v"),
-                )
+        def flip_w_bank(i, bank):
+            h, pair = bank // 2, bank % 2
+            s = i * HALVES + h
+            if pair == 0:
+                w_grouped = w_mid.tile([P, C, PAIR], F32, align_bytes=64)
+                w_grouped_of[s] = w_grouped
+            w_flip = flipped.tile([P, 2, PAIR, P], F32, tag="flip")
+            for a in range(2):
+                words = w_of[i][:, 2 * pair + a, :].bitcast(F32)
+                for v in range(PAIR):
+                    w0 = h * (C // PAIR) + v * P
+                    nc.tensor.transpose(w_flip[:, a, v, :], words[:, w0 : w0 + P], ident[:])
+            nc.scalar.copy(
+                out=w_grouped_of[s][:, 2 * pair * P : (2 * pair + 2) * P, :].rearrange("p (a c) v -> p a c v", a=2),
+                in_=w_flip[:].rearrange("p a v c -> p a c v"),
+            )
 
-        def quantise_w(s):
-            if 0 <= s < WINDOWS * PASSES:
+        def quantise_w(i, h):
+            if 0 <= i < W_TILES:
+                s = i * HALVES + h
                 nc.vector.quantize_mx(
                     out=w_codes[:, s, :].bitcast(E4M3X4),
                     scales=w_scales[:, s, :],
                     in_=w_grouped_of[s][:].rearrange("p c v -> p (c v)").bitcast(BF16),
                 )
 
-        def by_parity(channels):
-            return channels.rearrange("p (v q e) -> p v e q", v=2, e=2)
-
-        def in_blocks(channels):
-            return channels.rearrange("p (v e q) -> p v e q", v=2, e=2)
-
         def sigmoid(u):
             if is_unit(u):
                 sg = sig.tile([P, BRANCHES, C], F32)
                 for f in range(BRANCHES):
-                    nc.scalar.activation(out=in_blocks(sg[:, f, :]), in_=by_parity(pre_of[u][:, f, C : 2 * C]), func=ACT.Sigmoid)
+                    nc.scalar.activation(out=in_blocks(sg[:, f, :]), in_=as_in_dram(pre_of[u][:, f, C : 2 * C]), func=ACT.Sigmoid)
                 sg_of[u] = sg
 
-        def glu_of_branches(engine, u, first, last):
+        def glu_of_unit(u):
             if is_unit(u):
-                if first == 0:
-                    glu = double.tile([P, BRANCHES, C], F32)
-                    glu_of[u] = glu
-                for f in range(first, last + 1):
+                engine = nc.vector if u < VECTOR_GLU_UNITS else nc.gpsimd
+                glu = double.tile([P, BRANCHES, C], F32)
+                for f in range(BRANCHES):
                     engine.tensor_tensor(
-                        out=in_blocks(glu_of[u][:, f, :]), in0=by_parity(pre_of[u][:, f, 0:C]), in1=in_blocks(sg_of[u][:, f, :]), op=ALU.mult
+                        out=in_blocks(glu[:, f, :]), in0=as_in_dram(pre_of[u][:, f, 0:C]), in1=in_blocks(sg_of[u][:, f, :]), op=ALU.mult
                     )
+                glu_of[u] = glu
 
         def top_of_two(u):
             if is_unit(u):
@@ -149,31 +151,38 @@ def tile_stsindividuallayer_pb_v_kernel(tc, agg, W, b, pre, grad_out, out):
             if is_unit(u):
                 nc.vector.tensor_tensor(out=top_of[u][:], in0=top_of[u][:], in1=glu_of[u][:, 2, :], op=ALU.max)
 
-        def minus_top(u):
+        def negate_top(u):
             if is_unit(u):
-                minus = double.tile([P, C], F32)
-                nc.scalar.activation(out=minus[:], in_=top_of[u][:], func=ACT.Copy, scale=-1.0)
-                minus_of[u] = minus
+                minus_top = double.tile([P, C], F32)
+                nc.scalar.activation(out=minus_top[:], in_=top_of[u][:], func=ACT.Copy, scale=-1.0)
+                minus_top_of[u] = minus_top
 
         def flip_sg(u):
             if is_unit(u):
                 for f in range(BRANCHES):
                     sg_flipped = sg_banks.tile([P, PACK, P], F32)
                     for t in range(PACK):
-                        nc.tensor.transpose(sg_flipped[:, t, :], sg_of[u][:, f, t * P : (t + 1) * P], ident_f32[:])
+                        nc.tensor.transpose(sg_flipped[:, t, :], sg_of[u][:, f, t * P : (t + 1) * P], ident[:])
                     sg_flipped_of[(u, f)] = sg_flipped
+
+        def flip_minus_top(u):
+            if is_unit(u):
+                minus_top_flipped = flipped.tile([P, PACK, P], F32, tag="flip")
+                for t in range(PACK):
+                    nc.tensor.transpose(minus_top_flipped[:, t, :], minus_top_of[u][:, t * P : (t + 1) * P], ident[:])
+                minus_top_flipped_of[u] = minus_top_flipped
 
         def flip_gap(u, f):
             if is_unit(u):
                 if f == 0:
                     lost = double.tile([P, BRANCHES, P, PACK], BF16)
                     lost_of[u] = lost
-                bank = flipped.tile([P, PACK, P], F32, tag="flip")
+                gap = flipped.tile([P, PACK, P], F32, tag="flip")
                 for t in range(PACK):
-                    cols = slice(t * P, (t + 1) * P)
-                    nc.tensor.matmul(bank[:, t, :], lhsT=glu_of[u][:, f, cols], rhs=ident_f32[:], is_transpose=True, start=True, stop=False)
-                    nc.tensor.matmul(bank[:, t, :], lhsT=minus_of[u][:, cols], rhs=ident_f32[:], is_transpose=True, start=False, stop=True)
-                nc.scalar.activation(out=lost_of[u][:, f, :, :], in_=bank[:].rearrange("p t n -> p n t"), func=ACT.Sign)
+                    block = slice(t * P, (t + 1) * P)
+                    nc.tensor.matmul(gap[:, t, :], lhsT=glu_of[u][:, f, block], rhs=ident[:], is_transpose=True, start=True, stop=False)
+                    nc.tensor.matmul(gap[:, t, :], lhsT=minus_top_of[u][:, block], rhs=ident[:], is_transpose=True, start=False, stop=True)
+                nc.scalar.activation(out=lost_of[u][:, f, :, :], in_=gap[:].rearrange("p t n -> p n t"), func=ACT.Sign)
 
         def winners(u):
             if is_unit(u):
@@ -181,35 +190,28 @@ def tile_stsindividuallayer_pb_v_kernel(tc, agg, W, b, pre, grad_out, out):
                 nc.scalar.activation(out=won[:], in_=lost_of[u][:], func=ACT.Copy, bias=1.0)
                 won_of[u] = won
 
-        def flip_minus_top(u):
-            if is_unit(u):
-                bank = flipped.tile([P, PACK, P], F32, tag="flip")
-                for t in range(PACK):
-                    nc.tensor.transpose(bank[:, t, :], minus_of[u][:, t * P : (t + 1) * P], ident_f32[:])
-                minus_flipped_of[u] = bank
-
         def flip_grad(u):
             if is_unit(u):
-                bank = flipped.tile([P, 2, P], F32, tag="flip")
+                grad_flipped = flipped.tile([P, PAIR, P], F32, tag="flip")
                 words = grad[:, u, :].bitcast(F32)
-                for v in range(2):
-                    nc.tensor.transpose(bank[:, v, :], words[:, v * P : (v + 1) * P], ident_f32[:])
+                for v in range(PAIR):
+                    nc.tensor.transpose(grad_flipped[:, v, :], words[:, v * P : (v + 1) * P], ident[:])
                 half_grad = double.tile([P, P, PACK], F32)
                 nc.scalar.activation(
-                    out=half_grad[:].rearrange("p n (v e) -> p n v e", v=2),
-                    in_=bank[:].rearrange("p v n -> p (v n)").bitcast(BF16).rearrange("p (v n e) -> p n v e", v=2, e=2),
+                    out=half_grad[:].rearrange("p n (v e) -> p n v e", v=PAIR),
+                    in_=grad_flipped[:].rearrange("p v n -> p (v n)").bitcast(BF16).rearrange("p (v n e) -> p n v e", v=PAIR, e=PAIR),
                     func=ACT.Copy,
                     scale=-0.5,
                 )
                 half_grad_of[u] = half_grad
 
-        def lost_two(u):
+        def losers_of_two(u):
             if is_unit(u):
                 losers = single.tile([P, P, PACK], BF16)
                 nc.vector.tensor_tensor(out=losers[:], in0=lost_of[u][:, 0, :, :], in1=lost_of[u][:, 1, :, :], op=ALU.add)
                 losers_of[u] = losers
 
-        def lost_three(u):
+        def losers_of_three(u):
             if is_unit(u):
                 nc.vector.tensor_tensor(out=losers_of[u][:], in0=losers_of[u][:], in1=lost_of[u][:, 2, :, :], op=ALU.add)
 
@@ -225,7 +227,7 @@ def tile_stsindividuallayer_pb_v_kernel(tc, agg, W, b, pre, grad_out, out):
             if is_unit(u):
                 minus_share_top = single.tile([P, P, PACK], F32)
                 nc.vector.tensor_tensor(
-                    out=minus_share_top[:], in0=minus_flipped_of[u][:].rearrange("p t n -> p n t"), in1=share_of[u][:], op=ALU.mult
+                    out=minus_share_top[:], in0=minus_top_flipped_of[u][:].rearrange("p t n -> p n t"), in1=share_of[u][:], op=ALU.mult
                 )
                 minus_share_top_of[u] = minus_share_top
 
@@ -269,68 +271,68 @@ def tile_stsindividuallayer_pb_v_kernel(tc, agg, W, b, pre, grad_out, out):
                 )
 
         def multiply(u):
-            if is_unit(u):
-                w, rows = window_and_rows(u)
-                acc = sums.tile([P, C], F32)
-                for s in range(PASSES):
-                    nc.tensor.matmul_mx(
-                        out=acc[:],
-                        lhsT=d_codes_of[u][:, s, :].bitcast(E5M2X4),
-                        lhsT_scale=d_scales_of[u][:, s, :],
-                        rhs=w_codes[:, w * PASSES + s, :].bitcast(E4M3X4),
-                        rhs_scale=w_scales[:, w * PASSES + s, :],
-                        start=(s == 0),
-                        stop=(s == PASSES - 1),
-                    )
-                result = mx.tile([P, C], F32)
-                nc.scalar.copy(out=result[:], in_=acc[:])
-                nc.scalar.dma_start(out=out[0, w, rows, :], in_=result[:])
+            w, rows = window_and_rows(u)
+            acc = sums.tile([P, C], F32)
+            for s in range(PASSES):
+                nc.tensor.matmul_mx(
+                    out=acc[:],
+                    lhsT=d_codes_of[u][:, s, :].bitcast(E5M2X4),
+                    lhsT_scale=d_scales_of[u][:, s, :],
+                    rhs=w_codes[:, w * PASSES + s, :].bitcast(E4M3X4),
+                    rhs_scale=w_scales[:, w * PASSES + s, :],
+                    start=(s == 0),
+                    stop=(s == PASSES - 1),
+                )
+            result = mx.tile([P, C], F32)
+            nc.scalar.copy(out=result[:], in_=acc[:])
+            nc.scalar.dma_start(out=out[0, w, rows, :], in_=result[:])
 
         load_pre(0)
         load_pre(1)
         nc.sync.dma_start(out=grad[:], in_=grad_out[0].rearrange("w (a p) c -> p (w a) c", p=P))
         load_pre(2)
         sigmoid(0)
-        for f in range(BRANCHES):
-            glu_of_branches(nc.vector, 0, f, f)
-        w_loads = {0: [0, 1, 2], 1: [3], 3: [4], 4: [5]}
-        multiplies = {5: [0], 6: [1], 7: [2], 8: [3, 4], 9: [5, 6], 10: [7]}
+        glu_of_unit(0)
+        waiting = []
         for r in range(ROUNDS):
             begun, gapped, shared, masked = r, r - 1, r - 2, r - 3
+            flipped_w, quantised_w = r - FIRST_W_ROUND, r - FIRST_W_ROUND - 1
             load_pre(r + PRE_TILES)
-            for i in w_loads.get(r, []):
-                load_w(i)
+            for i in range(W_TILES):
+                first_free = FIRST_W_ROUND + i - W_BUFFERS + 1
+                if r == (i // BRANCHES if i < W_BUFFERS else first_free):
+                    load_w(i)
             sigmoid(begun + 1)
             flip_sg(shared)
             flip_minus_top(shared)
             for f in range(BRANCHES):
                 flip_gap(gapped, f)
-            lost_two(shared)
+            losers_of_two(shared)
             top_of_two(begun)
-            lost_three(shared)
+            losers_of_three(shared)
             mask(masked, 0)
             share_of_grad(shared)
             mask(masked, 1)
             quantise_branch(masked, 0)
             mask(masked, 2)
             quantise_branch(masked, 1)
-            first_bank = (r - FIRST_W_ROUND) * W_BANKS_A_ROUND
-            quantise_w((first_bank - W_BANKS_A_ROUND) // 2)
+            quantise_w(quantised_w, 0)
             quantise_branch(masked, 2)
-            quantise_w((first_bank - W_BANKS_A_ROUND) // 2 + 1)
+            quantise_w(quantised_w, 1)
             top_of_three(begun)
-            minus_top(begun)
-            if is_unit(shared):
-                glu_of_branches(nc.gpsimd, begun + 1, 0, BRANCHES - 1)
-            else:
-                for f in range(BRANCHES):
-                    glu_of_branches(nc.vector, begun + 1, f, f)
+            negate_top(begun)
+            glu_of_unit(begun + 1)
             share_times_top(shared)
             for f in range(BRANCHES):
                 products(shared, f)
             winners(gapped)
-            for u in multiplies.get(r, []):
+            if is_unit(masked):
+                waiting.append(masked)
+            ready = [u for u in waiting if quantised_w >= (u // NODE_TILES + 1) * BRANCHES - 1]
+            for u in ready[: (1 if flipped_w < W_TILES else 2)]:
+                waiting.remove(u)
                 multiply(u)
-            for k in range(first_bank, first_bank + W_BANKS_A_ROUND):
-                flip_w_bank(k)
+            if 0 <= flipped_w < W_TILES:
+                for bank in range(W_BANKS_A_TILE):
+                    flip_w_bank(flipped_w, bank)
             flip_grad(gapped)

from contextlib import ExitStack

import concourse.mybir as mybir
from concourse.masks import make_identity

F32 = mybir.dt.float32
BF16 = mybir.dt.bfloat16
U32 = mybir.dt.uint32
U8 = mybir.dt.uint8
E4M3X4 = mybir.dt.float8_e4m3fn_x4
E5M2X4 = mybir.dt.float8_e5m2_x4
ALU = mybir.AluOpType
ACT = mybir.ActivationFunctionType

P = 128
PACK = 4
PAIR = 2
WINDOWS = 2
BRANCHES = 3
NODES = 512
C = 512
HALVES = 2
PASSES = BRANCHES * HALVES
NODE_TILES = NODES // P
CH_TILES = C // P
UNITS = WINDOWS * NODE_TILES
PRE_TILES = 3
VECTOR_GLU_UNITS = 3
W_TILES = WINDOWS * BRANCHES
W_BUFFERS = 4
W_BANKS_A_TILE = 4
FIRST_W_ROUND = 2
WAITING_UNITS = 4
ROUNDS = UNITS + 3

FLOPS = 2 * WINDOWS * NODES * C * BRANCHES * 2 * C
BYTES = WINDOWS * (BRANCHES * NODES * 2 * C * 4 + BRANCHES * C * 2 * C * 2 + NODES * C * 2 + NODES * C * 4)


def is_unit(u):
    return 0 <= u < UNITS


def window_and_rows(u):
    return u // NODE_TILES, slice((u % NODE_TILES) * P, (u % NODE_TILES + 1) * P)


def as_in_dram(channels):
    return channels.rearrange("p (v q e) -> p v e q", v=PAIR, e=PAIR)


def in_blocks(channels):
    return channels.rearrange("p (v e q) -> p v e q", v=PAIR, e=PAIR)


def tile_stsindividuallayer_pb_v_kernel(tc, agg, W, b, pre, grad_out, out):
    nc = tc.nc
    with ExitStack() as stack:
        keep = stack.enter_context(tc.tile_pool(name="keep", bufs=1))
        pre_in = stack.enter_context(tc.tile_pool(name="pre_in", bufs=PRE_TILES))
        w_in = stack.enter_context(tc.tile_pool(name="w_in", bufs=W_BUFFERS))
        sig = stack.enter_context(tc.tile_pool(name="sig", bufs=4))
        single = stack.enter_context(tc.tile_pool(name="single", bufs=1))
        double = stack.enter_context(tc.tile_pool(name="double", bufs=2))
        triple = stack.enter_context(tc.tile_pool(name="triple", bufs=3))
        w_mid = stack.enter_context(tc.tile_pool(name="w_mid", bufs=2 * HALVES))
        mx = stack.enter_context(tc.tile_pool(name="mx", bufs=WAITING_UNITS))
        sg_banks = stack.enter_context(tc.psum_pool(name="sg_banks", bufs=BRANCHES))
        flipped = stack.enter_context(tc.psum_pool(name="flipped", bufs=4))
        sums = stack.enter_context(tc.psum_pool(name="sums", bufs=1))

        ident = keep.tile([P, P], F32)
        make_identity(nc, ident[:])

        grad = keep.tile([P, UNITS, C], BF16)
        w_codes = keep.tile([P, WINDOWS * PASSES, C], U32, align_bytes=64)
        w_scales = keep.tile([P, WINDOWS * PASSES, C], U8, align_bytes=64)
        pre_of, w_of, w_grouped_of = {}, {}, {}
        sg_of, glu_of, top_of, minus_top_of = {}, {}, {}, {}
        sg_flipped_of, minus_top_flipped_of, lost_of, won_of = {}, {}, {}, {}
        losers_of, half_grad_of, share_of, minus_share_top_of = {}, {}, {}, {}
        dpre_of, d_codes_of, d_scales_of = {}, {}, {}

        def load_pre(u):
            if is_unit(u):
                w, rows = window_and_rows(u)
                pre_t = pre_in.tile([P, BRANCHES, 2 * C], F32)
                for f in range(BRANCHES):
                    if u == 0:
                        nc.sync.dma_start(out=pre_t[:, f, C : 2 * C], in_=pre[0, w, f, rows, C : 2 * C])
                        nc.sync.dma_start(out=pre_t[:, f, 0:C], in_=pre[0, w, f, rows, 0:C])
                    else:
                        nc.sync.dma_start(out=pre_t[:, f, :], in_=pre[0, w, f, rows, :])
                pre_of[u] = pre_t

        def load_w(i):
            w_raw = w_in.tile([P, CH_TILES, 2 * C], BF16)
            nc.sync.dma_start(out=w_raw[:], in_=W[i // BRANCHES, i % BRANCHES].rearrange("(a p) j -> p a j", p=P))
            w_of[i] = w_raw

        def flip_w_bank(i, bank):
            h, pair = bank // 2, bank % 2
            s = i * HALVES + h
            if pair == 0:
                w_grouped = w_mid.tile([P, C, PAIR], F32, align_bytes=64)
                w_grouped_of[s] = w_grouped
            w_flip = flipped.tile([P, 2, PAIR, P], F32, tag="flip")
            for a in range(2):
                words = w_of[i][:, 2 * pair + a, :].bitcast(F32)
                for v in range(PAIR):
                    w0 = h * (C // PAIR) + v * P
                    nc.tensor.transpose(w_flip[:, a, v, :], words[:, w0 : w0 + P], ident[:])
            nc.scalar.copy(
                out=w_grouped_of[s][:, 2 * pair * P : (2 * pair + 2) * P, :].rearrange("p (a c) v -> p a c v", a=2),
                in_=w_flip[:].rearrange("p a v c -> p a c v"),
            )

        def quantise_w(i, h):
            if 0 <= i < W_TILES:
                s = i * HALVES + h
                nc.vector.quantize_mx(
                    out=w_codes[:, s, :].bitcast(E4M3X4),
                    scales=w_scales[:, s, :],
                    in_=w_grouped_of[s][:].rearrange("p c v -> p (c v)").bitcast(BF16),
                )

        def sigmoid(u):
            if is_unit(u):
                sg = sig.tile([P, BRANCHES, C], F32)
                for f in range(BRANCHES):
                    nc.scalar.activation(out=in_blocks(sg[:, f, :]), in_=as_in_dram(pre_of[u][:, f, C : 2 * C]), func=ACT.Sigmoid)
                sg_of[u] = sg

        def glu_of_unit(u):
            if is_unit(u):
                engine = nc.vector if u < VECTOR_GLU_UNITS else nc.gpsimd
                glu = double.tile([P, BRANCHES, C], F32)
                for f in range(BRANCHES):
                    engine.tensor_tensor(
                        out=in_blocks(glu[:, f, :]), in0=as_in_dram(pre_of[u][:, f, 0:C]), in1=in_blocks(sg_of[u][:, f, :]), op=ALU.mult
                    )
                glu_of[u] = glu

        def top_of_two(u):
            if is_unit(u):
                top = double.tile([P, C], F32)
                nc.vector.tensor_tensor(out=top[:], in0=glu_of[u][:, 0, :], in1=glu_of[u][:, 1, :], op=ALU.max)
                top_of[u] = top

        def top_of_three(u):
            if is_unit(u):
                nc.vector.tensor_tensor(out=top_of[u][:], in0=top_of[u][:], in1=glu_of[u][:, 2, :], op=ALU.max)

        def negate_top(u):
            if is_unit(u):
                minus_top = double.tile([P, C], F32)
                nc.scalar.activation(out=minus_top[:], in_=top_of[u][:], func=ACT.Copy, scale=-1.0)
                minus_top_of[u] = minus_top

        def flip_sg(u):
            if is_unit(u):
                for f in range(BRANCHES):
                    sg_flipped = sg_banks.tile([P, PACK, P], F32)
                    for t in range(PACK):
                        nc.tensor.transpose(sg_flipped[:, t, :], sg_of[u][:, f, t * P : (t + 1) * P], ident[:])
                    sg_flipped_of[(u, f)] = sg_flipped

        def flip_minus_top(u):
            if is_unit(u):
                minus_top_flipped = flipped.tile([P, PACK, P], F32, tag="flip")
                for t in range(PACK):
                    nc.tensor.transpose(minus_top_flipped[:, t, :], minus_top_of[u][:, t * P : (t + 1) * P], ident[:])
                minus_top_flipped_of[u] = minus_top_flipped

        def flip_gap(u, f):
            if is_unit(u):
                if f == 0:
                    lost = double.tile([P, BRANCHES, P, PACK], BF16)
                    lost_of[u] = lost
                gap = flipped.tile([P, PACK, P], F32, tag="flip")
                for t in range(PACK):
                    block = slice(t * P, (t + 1) * P)
                    nc.tensor.matmul(gap[:, t, :], lhsT=glu_of[u][:, f, block], rhs=ident[:], is_transpose=True, start=True, stop=False)
                    nc.tensor.matmul(gap[:, t, :], lhsT=minus_top_of[u][:, block], rhs=ident[:], is_transpose=True, start=False, stop=True)
                nc.scalar.activation(out=lost_of[u][:, f, :, :], in_=gap[:].rearrange("p t n -> p n t"), func=ACT.Sign)

        def winners(u):
            if is_unit(u):
                won = triple.tile([P, BRANCHES, P, PACK], BF16)
                nc.scalar.activation(out=won[:], in_=lost_of[u][:], func=ACT.Copy, bias=1.0)
                won_of[u] = won

        def flip_grad(u):
            if is_unit(u):
                grad_flipped = flipped.tile([P, PAIR, P], F32, tag="flip")
                words = grad[:, u, :].bitcast(F32)
                for v in range(PAIR):
                    nc.tensor.transpose(grad_flipped[:, v, :], words[:, v * P : (v + 1) * P], ident[:])
                half_grad = double.tile([P, P, PACK], F32)
                nc.scalar.activation(
                    out=half_grad[:].rearrange("p n (v e) -> p n v e", v=PAIR),
                    in_=grad_flipped[:].rearrange("p v n -> p (v n)").bitcast(BF16).rearrange("p (v n e) -> p n v e", v=PAIR, e=PAIR),
                    func=ACT.Copy,
                    scale=-0.5,
                )
                half_grad_of[u] = half_grad

        def losers_of_two(u):
            if is_unit(u):
                losers = single.tile([P, P, PACK], BF16)
                nc.vector.tensor_tensor(out=losers[:], in0=lost_of[u][:, 0, :, :], in1=lost_of[u][:, 1, :, :], op=ALU.add)
                losers_of[u] = losers

        def losers_of_three(u):
            if is_unit(u):
                nc.vector.tensor_tensor(out=losers_of[u][:], in0=losers_of[u][:], in1=lost_of[u][:, 2, :, :], op=ALU.add)

        def share_of_grad(u):
            if is_unit(u):
                share = single.tile([P, P, PACK], F32)
                nc.vector.scalar_tensor_tensor(
                    out=share[:], in0=losers_of[u][:], scalar=-2.0 / 3.0, in1=half_grad_of[u][:], op0=ALU.min, op1=ALU.mult
                )
                share_of[u] = share

        def share_times_top(u):
            if is_unit(u):
                minus_share_top = single.tile([P, P, PACK], F32)
                nc.vector.tensor_tensor(
                    out=minus_share_top[:], in0=minus_top_flipped_of[u][:].rearrange("p t n -> p n t"), in1=share_of[u][:], op=ALU.mult
                )
                minus_share_top_of[u] = minus_share_top

        def products(u, f):
            if is_unit(u):
                if f == 0:
                    dpre = single.tile([P, BRANCHES, HALVES, P, PACK], BF16, align_bytes=64)
                    dpre_of[u] = dpre
                sg_by_node = sg_flipped_of[(u, f)][:].rearrange("p t n -> p n t")
                nc.vector.tensor_tensor(out=dpre_of[u][:, f, 0, :, :], in0=sg_by_node, in1=share_of[u][:], op=ALU.mult)
                nc.vector.scalar_tensor_tensor(
                    out=dpre_of[u][:, f, 1, :, :],
                    in0=sg_by_node,
                    scalar=1.0,
                    in1=minus_share_top_of[u][:],
                    op0=ALU.subtract,
                    op1=ALU.mult,
                )

        def mask(u, f):
            if is_unit(u):
                both_halves = dpre_of[u][:, f, :, :, :].rearrange("p h n t -> p h (n t)")
                nc.vector.tensor_tensor(
                    out=both_halves,
                    in0=both_halves,
                    in1=won_of[u][:, f, :, :].rearrange("p n t -> p (n t)").unsqueeze(1).to_broadcast([P, HALVES, C]),
                    op=ALU.mult,
                )

        def quantise_branch(u, f):
            if is_unit(u):
                if f == 0:
                    d_codes = mx.tile([P, PASSES, P], U32, align_bytes=64)
                    d_scales = mx.tile([P, PASSES, P], U8, align_bytes=64)
                    d_codes_of[u], d_scales_of[u] = d_codes, d_scales
                both = slice(f * HALVES, (f + 1) * HALVES)
                nc.vector.quantize_mx(
                    out=d_codes_of[u][:, both, :].rearrange("p h n -> p (h n)").bitcast(E5M2X4),
                    scales=d_scales_of[u][:, both, :].rearrange("p h n -> p (h n)"),
                    in_=dpre_of[u][:, f, :, :, :].rearrange("p h n t -> p (h n t)"),
                )

        def multiply(u):
            w, rows = window_and_rows(u)
            acc = sums.tile([P, C], F32)
            for s in range(PASSES):
                nc.tensor.matmul_mx(
                    out=acc[:],
                    lhsT=d_codes_of[u][:, s, :].bitcast(E5M2X4),
                    lhsT_scale=d_scales_of[u][:, s, :],
                    rhs=w_codes[:, w * PASSES + s, :].bitcast(E4M3X4),
                    rhs_scale=w_scales[:, w * PASSES + s, :],
                    start=(s == 0),
                    stop=(s == PASSES - 1),
                )
            result = mx.tile([P, C], F32)
            nc.scalar.copy(out=result[:], in_=acc[:])
            nc.scalar.dma_start(out=out[0, w, rows, :], in_=result[:])

        load_pre(0)
        load_pre(1)
        nc.sync.dma_start(out=grad[:], in_=grad_out[0].rearrange("w (a p) c -> p (w a) c", p=P))
        load_pre(2)
        sigmoid(0)
        glu_of_unit(0)
        waiting = []
        for r in range(ROUNDS):
            begun, gapped, shared, masked = r, r - 1, r - 2, r - 3
            flipped_w, quantised_w = r - FIRST_W_ROUND, r - FIRST_W_ROUND - 1
            load_pre(r + PRE_TILES)
            for i in range(W_TILES):
                first_free = FIRST_W_ROUND + i - W_BUFFERS + 1
                if r == (i // BRANCHES if i < W_BUFFERS else first_free):
                    load_w(i)
            sigmoid(begun + 1)
            flip_sg(shared)
            flip_minus_top(shared)
            for f in range(BRANCHES):
                flip_gap(gapped, f)
            losers_of_two(shared)
            top_of_two(begun)
            losers_of_three(shared)
            mask(masked, 0)
            share_of_grad(shared)
            mask(masked, 1)
            quantise_branch(masked, 0)
            mask(masked, 2)
            quantise_branch(masked, 1)
            quantise_w(quantised_w, 0)
            quantise_branch(masked, 2)
            quantise_w(quantised_w, 1)
            top_of_three(begun)
            negate_top(begun)
            glu_of_unit(begun + 1)
            share_times_top(shared)
            for f in range(BRANCHES):
                products(shared, f)
            winners(gapped)
            if is_unit(masked):
                waiting.append(masked)
            ready = [u for u in waiting if quantised_w >= (u // NODE_TILES + 1) * BRANCHES - 1]
            for u in ready[: (1 if flipped_w < W_TILES else 2)]:
                waiting.remove(u)
                multiply(u)
            if 0 <= flipped_w < W_TILES:
                for bank in range(W_BANKS_A_TILE):
                    flip_w_bank(flipped_w, bank)
            flip_grad(gapped)
